import numpy as np
import ml_dtypes


def mxq(x, axis, fmt="e4m3"):
    dtype, down = {"e4m3": (ml_dtypes.float8_e4m3fn, 7), "e5m2": (ml_dtypes.float8_e5m2, 14)}[fmt]
    v = np.moveaxis(np.asarray(x, np.float32).astype(ml_dtypes.bfloat16).astype(np.float64), axis, -1)
    blocks = v.reshape(v.shape[:-1] + (-1, 32))
    amax = np.abs(blocks).max(-1, keepdims=True)
    byte = np.maximum(np.where(amax > 0, np.frexp(amax)[1] - 1 + 127, 0) - down, 1)
    scale = np.exp2(byte - 127.0)
    codes = (blocks / scale).astype(np.float32).astype(dtype).astype(np.float64)
    return np.moveaxis((codes * scale).reshape(v.shape), -1, axis)


WIDE = False


def mx_kscale(k):
    if not WIDE:
        return np.ones(k)
    levels = np.array([18, -18])
    if k % 512:
        return np.exp2(np.random.permutation(np.resize(levels, k // 32))).repeat(32)
    a = np.empty((k // 512, 16))
    for p in range(k // 512):
        a[p, :8] = np.random.permutation(np.resize(levels, 8))
        for g in range(8):
            far = levels[np.abs(levels - a[p, g]) >= 10]
            a[p, g + 8] = far[np.random.randint(len(far))]
    return np.exp2(a.ravel()).repeat(32)


BF16 = ml_dtypes.bfloat16


def bf(x):
    return np.asarray(x, np.float32).astype(BF16)


def f64(x):
    return np.asarray(x).astype(np.float64)


B, N, R, I = 2, 2048, 128, 512
SIG = 1.5
P0 = 0.05
RM = np.exp(0.5 * SIG * SIG)


def draw_flows():
    keep = np.random.random((B, 1, N)) >= P0
    return keep * np.exp(SIG * np.random.standard_normal((B, N, N)) - 0.5 * SIG * SIG)


def inv_sqrt_degree(flows):
    deg = f64(flows).sum(axis=1)
    return np.where(deg > 0, 1.0 / np.sqrt(np.where(deg > 0, deg, 1.0)), 0.0)


def setup_inputs():
    u = mx_kscale(N)
    v = mx_kscale(I)
    s = mx_kscale(B * N).reshape(B, N)
    flows0 = bf(draw_flows())
    x0 = bf(np.random.standard_normal((B, N, R)))
    W2_0 = bf(np.random.standard_normal((R, I)) * 0.5 * np.sqrt(N) / (RM * np.sqrt(R)))
    b2 = bf(np.random.standard_normal(I) * 0.1)
    g = bf(np.random.standard_normal((B, N, I)) * np.exp2(np.random.randint(-6, 1, (B, N, 1))) * 4.0 * u[None, :, None] * v)
    dinv = inv_sqrt_degree(flows0)
    return {"flows": bf(f64(flows0) / s[:, :, None] / u[None, None, :]),
            "x_gcn1": bf(f64(x0) * s[:, :, None]),
            "W2": bf(f64(W2_0) / v),
            "b2": b2,
            "dinv": np.asarray(dinv, np.float32),
            "grad_out": g}


def reference(flows, x_gcn1, W2, b2, dinv, grad_out):
    di = f64(dinv)[..., None]
    gz = f64(grad_out) * di
    dmsg = mxq(f64(flows), 2, "e4m3") @ mxq(gz, 1, "e5m2")
    dxw = (dmsg * di).reshape(B * N, I)
    dx = mxq(dxw, 1, "e5m2") @ mxq(f64(W2), 1, "e4m3").T
    dW2 = mxq(f64(x_gcn1).reshape(B * N, R), 0, "e4m3").T @ mxq(dxw, 0, "e5m2")
    return dx.reshape(B, N, R), dW2

@@ -1,0 +1,378 @@
+from contextlib import ExitStack
+
+import concourse.mybir as mybir
+from concourse.masks import make_identity
+
+F32 = mybir.dt.float32
+BF16 = mybir.dt.bfloat16
+U32 = mybir.dt.uint32
+I32 = mybir.dt.int32
+U8 = mybir.dt.uint8
+E4 = mybir.dt.float8_e4m3fn_x4
+E5 = mybir.dt.float8_e5m2_x4
+COPY = mybir.ActivationFunctionType.Copy
+MULT = mybir.AluOpType.mult
+
+B, N, R, I = 2, 2048, 128, 512
+P = 128
+NG = N // 512
+PAIRS = B * N // 256
+GROUPS = B * N // 512
+
+FLOPS = 2 * B * N * N * I + 2 * 2 * B * N * I * R
+
+PERM = {(k, s) for k in range(3, PAIRS) for s in range(2)} - {(6, 1), (8, 0), (8, 1)}
+
+
+def tile_encoder_flows_pb_v_kernel(tc, flows, x_gcn1, W2, b2, dinv, grad_out, out_0, out_1):
+    nc = tc.nc
+    with ExitStack() as ctx:
+        keep = ctx.enter_context(tc.tile_pool(name="keep", bufs=1))
+        work = ctx.enter_context(tc.tile_pool(name="work", bufs=2))
+        tpool = ctx.enter_context(tc.psum_pool(name="tpool", bufs=4))
+        apool = ctx.enter_context(tc.psum_pool(name="apool", bufs=4))
+        ctx.enter_context(tc.manual_schedule())
+
+        ident = keep.tile([P, P], F32, name="ident", align_bytes=64)
+        make_identity(nc, ident[:])
+        dv = keep.tile([P, GROUPS, 4], F32, name="dv", align_bytes=64)
+        wcodes = keep.tile([P, 896], U32, name="wcodes", align_bytes=64)
+        wscale = keep.tile([P, 896], U8, name="wscale", align_bytes=64)
+        nc.gpsimd.memset(wcodes[:].bitcast(I32), 0)
+        nc.gpsimd.memset(wscale[:].bitcast(I32), 0)
+
+        raw, perm, ft, fc, fs, gr, gm, gi, gc, gs = {}, {}, {}, {}, {}, {}, {}, {}, {}, {}
+        bank, acc, D, dtb, dtbank, dtc, dts, DI, tcod, tscl = {}, {}, {}, {}, {}, {}, {}, {}, {}, {}
+        misc = {}
+
+        def load_dv():
+            nc.scalar.dma_start(out=dv[:], in_=dinv.rearrange("b (g p t) -> p (b g) t", p=P, t=4))
+
+        def load_flows(k, s=None):
+            if k not in raw:
+                raw[k] = work.tile([P, 2, N], BF16, name="raw", bufs=6, align_bytes=64)
+            b, rest = divmod(k, PAIRS // B)
+            g, h = divmod(rest, 2)
+            src = flows[b, 512 * g:512 * (g + 1), :].rearrange("(p t) c -> p t c", t=4)
+            if s is None:
+                nc.sync.dma_start(out=raw[k][:], in_=src[:, 2 * h:2 * h + 2, :])
+            else:
+                nc.sync.dma_start(out=raw[k][:, s, :], in_=src[:, 2 * h + s, :])
+
+        def load_grad(b, g):
+            gr[b, g] = work.tile([P, 4, I], BF16, name="gr", bufs=4, align_bytes=64)
+            nc.sync.dma_start(out=gr[b, g][:], in_=grad_out[b, 512 * g:512 * (g + 1), :].rearrange("(p j) w -> p j w", j=4))
+
+        def load_w():
+            misc["w"] = keep.tile([P, I], BF16, name="wraw", align_bytes=64)
+            nc.sync.dma_start(out=misc["w"][:], in_=W2)
+
+        def load_x():
+            misc["x"] = keep.tile([P, GROUPS, 4, R], BF16, name="xraw", align_bytes=64)
+            for b in range(B):
+                nc.sync.dma_start(out=misc["x"][:, 4 * b:4 * b + 4], in_=x_gcn1[b].rearrange("(g p t) w -> p g t w", p=P, t=4))
+
+        def gz_mul(b, g, js=(0, 1, 2, 3)):
+            if (b, g) not in gm:
+                gm[b, g] = work.tile([P, 4, I], BF16, name="gm", bufs=3, align_bytes=64)
+            for j in js:
+                nc.vector.tensor_scalar(out=gm[b, g][:, j, :], in0=gr[b, g][:, j, :],
+                                        scalar1=dv[:, 4 * b + g, j:j + 1], scalar2=None, op0=MULT)
+
+        def gz_int(b, g, u, eng="v"):
+            if (b, g) not in gi:
+                gi[b, g] = work.tile([P, 4 * I], BF16, name="gi", bufs=2, align_bytes=64)
+            out = gi[b, g][:, 1024 * u:1024 * (u + 1)].rearrange("p (m e j) -> p m e j", e=2, j=4)
+            src = gm[b, g][:].rearrange("p j (m u e) -> p u m e j", u=2, e=2)[:, u]
+            if eng == "v":
+                nc.vector.tensor_copy(out=out, in_=src)
+            else:
+                nc.scalar.copy(out=out, in_=src)
+
+        def gz_q(b, g):
+            gc[b, g] = keep.tile([P, I], U32, name="gc%d%d" % (b, g), align_bytes=64)
+            gs[b, g] = keep.tile([P, I], U8, name="gs%d%d" % (b, g), align_bytes=64)
+            nc.vector.quantize_mx(out=gc[b, g][:].bitcast(E5), scales=gs[b, g][:], in_=gi[b, g][:])
+
+        def sort_words(k, s):
+            if (k, s) in PERM:
+                perm[k, s] = work.tile([P, NG, 2, P], F32, name="perm", bufs=3, align_bytes=64)
+                nc.vector.tensor_copy(out=perm[k, s][:],
+                                      in_=raw[k][:, s, :].bitcast(F32).rearrange("p (g m u) -> p g u m", g=NG, u=2))
+
+        def tr(k, s, h):
+            ps = tpool.tile([P, 4, P], F32, name="ps")
+            bank[k, s, h] = ps
+            words = raw[k][:, s, :].bitcast(F32)
+            for q in range(4):
+                g, u = 2 * h + q // 2, q % 2
+                if (k, s) in PERM:
+                    src = perm[k, s][:, g, u, :]
+                else:
+                    src = words[:, 256 * g + u:256 * (g + 1):2]
+                nc.tensor.transpose(ps[:, q, :], src, ident[:])
+
+        def tr_copy(k, s, h, eng="s"):
+            if (k, s) not in ft:
+                ft[k, s] = work.tile([P, 4 * NG * P], BF16, name="ft", bufs=5, align_bytes=64)
+            out = ft[k, s][:].bitcast(F32)[:, 512 * h:512 * (h + 1)].rearrange("p (g r u) -> p g r u", g=2, u=2)
+            src = bank[k, s, h][:].rearrange("p (g u) r -> p g r u", u=2)
+            if eng == "s":
+                nc.scalar.copy(out=out, in_=src)
+            else:
+                nc.vector.tensor_copy(out=out, in_=src)
+
+        def quant(k, s):
+            fc[k, s] = work.tile([P, NG * P], U32, name="fc", bufs=6, align_bytes=64)
+            fs[k, s] = work.tile([P, NG * P], U8, name="fs", bufs=6, align_bytes=64)
+            nc.vector.quantize_mx(out=fc[k, s][:].bitcast(E4), scales=fs[k, s][:], in_=ft[k, s][:])
+
+        def mm(k, s, g):
+            b = k // (PAIRS // B)
+            if g == 0:
+                acc[k, s] = apool.tile([P, I], F32, name="acc")
+            cols = slice(P * g, P * (g + 1))
+            nc.tensor.matmul_mx(out=acc[k, s][:], lhsT=fc[k, s][:, cols].bitcast(E4), lhsT_scale=fs[k, s][:, cols],
+                                rhs=gc[b, g][:].bitcast(E5), rhs_scale=gs[b, g][:], start=(g == 0), stop=(g == NG - 1))
+
+        def dxw(k, s, eng="s", half=None):
+            G, t = divmod(2 * k + s, 4)
+            if G not in D:
+                D[G] = work.tile([P, 4, I], BF16, name="D", bufs=3, align_bytes=64)
+            cols = slice(0, I) if half is None else slice(256 * half, 256 * (half + 1))
+            if eng == "s":
+                nc.scalar.activation(out=D[G][:, t, cols], in_=acc[k, s][:, cols], func=COPY, scale=dv[:, G, t:t + 1])
+            else:
+                nc.vector.tensor_scalar(out=D[G][:, t, cols], in0=acc[k, s][:, cols], scalar1=dv[:, G, t:t + 1],
+                                        scalar2=None, op0=MULT)
+
+        def dt(k, slots=(0, 1)):
+            if k not in dtbank:
+                ps = tpool.tile([P, 4, P], F32, name="ps")
+                dtbank[k] = ps
+            ps = dtbank[k]
+            for s in slots:
+                G, t = divmod(2 * k + s, 4)
+                words = D[G][:, t, :].bitcast(F32)
+                for u in range(2):
+                    nc.tensor.transpose(ps[:, 2 * s + u, :], words[:, P * u:P * (u + 1)], ident[:])
+
+        def dt_copy(k, slots=slice(0, 2), eng="s"):
+            if k not in dtb:
+                dtb[k] = work.tile([P, 1024], BF16, name="dtb", bufs=3, align_bytes=64)
+            out = dtb[k][:].bitcast(F32).rearrange("p (v r u) -> p v r u", v=2, u=2)[:, slots]
+            src = dtbank[k][:].rearrange("p (v u) r -> p v r u", u=2)[:, slots]
+            if eng == "s":
+                nc.scalar.copy(out=out, in_=src)
+            else:
+                nc.vector.tensor_copy(out=out, in_=src)
+
+        def dt_q(k, a=0, z=2):
+            if k not in dtc:
+                dtc[k] = work.tile([P, 256], U32, name="dtc", bufs=4, align_bytes=64)
+                dts[k] = work.tile([P, 256], U8, name="dts", bufs=4, align_bytes=64)
+            nc.vector.quantize_mx(out=dtc[k][:, P * a:P * z].bitcast(E5), scales=dts[k][:, P * a:P * z], in_=dtb[k][:, 512 * a:512 * z])
+
+        def dx(G):
+            ps = apool.tile([P, I], F32, name="acc")
+            acc["dx", G] = ps
+            for t in range(4):
+                k, s = 2 * G + t // 2, t % 2
+                cols = slice(P * s, P * (s + 1))
+                win = slice(384 - P * t, 896 - P * t)
+                nc.tensor.matmul_mx(out=ps[:], lhsT=dtc[k][:, cols].bitcast(E5), lhsT_scale=dts[k][:, cols],
+                                    rhs=wcodes[:, win].bitcast(E4), rhs_scale=wscale[:, win], start=(t == 0), stop=(t == 3))
+
+        def dx_out(G, eng="s"):
+            ob = work.tile([P, I], F32, name="ob", bufs=2, align_bytes=64)
+            if eng == "s":
+                nc.scalar.copy(out=ob[:], in_=acc["dx", G][:])
+            else:
+                nc.vector.tensor_copy(out=ob[:], in_=acc["dx", G][:])
+            b, g = divmod(G, GROUPS // B)
+            dst = out_0[b, 512 * g:512 * (g + 1), :].rearrange("(p t) w -> p t w", t=4)
+            nc.sync.dma_start(out=dst, in_=ob[:].rearrange("p (t w) -> p t w", t=4))
+
+        def tok(G, h, eng="v"):
+            if G not in DI:
+                DI[G] = work.tile([P, 4 * I], BF16, name="DI", bufs=2, align_bytes=64)
+            out = DI[G][:, 1024 * h:1024 * (h + 1)].rearrange("p (n t) -> p n t", t=4)
+            src = D[G][:, :, 256 * h:256 * (h + 1)].rearrange("p t n -> p n t")
+            if eng == "v":
+                nc.vector.tensor_copy(out=out, in_=src)
+            else:
+                nc.scalar.copy(out=out, in_=src)
+
+        def tok_q(G):
+            tcod[G] = keep.tile([P, I], U32, name="tc%d" % G, align_bytes=64)
+            tscl[G] = keep.tile([P, I], U8, name="ts%d" % G, align_bytes=64)
+            nc.vector.quantize_mx(out=tcod[G][:].bitcast(E5), scales=tscl[G][:], in_=DI[G][:])
+
+        def x_int(b, part):
+            if "xi" not in misc:
+                misc["xi"] = keep.tile([P, GROUPS, R, 4], BF16, name="xi", align_bytes=64)
+            nc.vector.tensor_copy(out=misc["xi"][:, 4 * b + part:4 * b + part + 1], in_=misc["x"][:, 4 * b + part:4 * b + part + 1].rearrange("p g t w -> p g w t"))
+
+        def x_q():
+            misc["xc"] = keep.tile([P, GROUPS * R], U32, name="xc", align_bytes=64)
+            misc["xs"] = keep.tile([P, GROUPS * R], U8, name="xs", align_bytes=64)
+            nc.vector.quantize_mx(out=misc["xc"][:].bitcast(E4), scales=misc["xs"][:], in_=misc["xi"][:].rearrange("p g w t -> p (g w t)"))
+
+        def dw(G):
+            if G == 0:
+                acc["dw"] = apool.tile([P, I], F32, name="acc")
+            cols = slice(R * G, R * (G + 1))
+            nc.tensor.matmul_mx(out=acc["dw"][:], lhsT=misc["xc"][:, cols].bitcast(E4), lhsT_scale=misc["xs"][:, cols],
+                                rhs=tcod[G][:].bitcast(E5), rhs_scale=tscl[G][:], start=(G == 0), stop=(G == GROUPS - 1))
+
+        def dw_out():
+            wo = work.tile([P, I], F32, name="ob", bufs=2, align_bytes=64)
+            nc.vector.tensor_copy(out=wo[:].rearrange("p (m u e) -> p m u e", u=2, e=2),
+                                  in_=acc["dw"][:].rearrange("p (u m e) -> p m u e", u=2, e=2))
+            nc.sync.dma_start(out=out_1, in_=wo[:])
+
+        def w_tr():
+            ps = tpool.tile([P, 4, P], F32, name="ps")
+            misc["wps"] = ps
+            words = misc["w"][:].bitcast(F32)
+            for u in range(2):
+                nc.tensor.transpose(ps[:, u, :], words[:, u:256:2], ident[:])
+
+        def w_copy():
+            misc["wi"] = keep.tile([P, 4 * R], BF16, name="wi", align_bytes=64)
+            nc.scalar.copy(out=misc["wi"][:].bitcast(F32).rearrange("p (r u) -> p r u", u=2),
+                           in_=misc["wps"][:, 0:2, :].rearrange("p u r -> p r u"))
+
+        def w_q():
+            nc.vector.quantize_mx(out=wcodes[:, 384:512].bitcast(E4), scales=wscale[:, 384:512], in_=misc["wi"][:])
+
+        load_dv()
+        load_grad(0, 0)
+        load_flows(0, 0)
+        load_grad(0, 1)
+        load_flows(0, 1)
+        load_grad(0, 2)
+        load_grad(0, 3)
+        load_flows(1)
+        load_flows(2)
+        load_w()
+        load_flows(3)
+        load_flows(4)
+        load_x()
+
+        def trs(k, s):
+            for h in range(2):
+                tr(k, s, h)
+                tr_copy(k, s, h)
+
+        def mms(slots, gs_):
+            for g in gs_:
+                for k, s in slots:
+                    mm(k, s, g)
+
+        gz_mul(0, 0)
+        gz_int(0, 0, 0)
+        gz_int(0, 0, 1)
+        trs(0, 0)
+        gz_mul(0, 1)
+        gz_q(0, 0)
+        trs(0, 1)
+        gz_int(0, 1, 0)
+        gz_int(0, 1, 1, "s")
+        quant(0, 0)
+        gz_mul(0, 2)
+        gz_mul(0, 3)
+        gz_int(0, 2, 0, "s")
+        gz_int(0, 2, 1)
+        gz_q(0, 1)
+        quant(0, 1)
+        gz_int(0, 3, 0)
+        gz_q(0, 2)
+        gz_int(0, 3, 1)
+        mms([(0, 0), (0, 1)], (0, 1))
+        trs(1, 0)
+        trs(1, 1)
+        mms([(0, 0), (0, 1)], (2,))
+        gz_q(0, 3)
+        mms([(0, 0), (0, 1)], (3,))
+        quant(1, 0)
+        sort_words(3, 0)
+        quant(1, 1)
+        dxw(0, 0)
+        dxw(0, 1)
+        trs(2, 0)
+        trs(2, 1)
+        sort_words(3, 1)
+        mms([(1, 0)], range(4))
+        mms([(1, 1)], range(4))
+        quant(2, 0)
+        quant(2, 1)
+        dxw(1, 0)
+        dxw(1, 1)
+        w_tr()
+        w_copy()
+
+        gz1 = []
+        for g in range(NG):
+            gz1 += [lambda g=g: gz_mul(1, g), lambda g=g: gz_int(1, g, 0), lambda g=g: gz_int(1, g, 1), lambda g=g: gz_q(1, g)]
+        for k in range(3, PAIRS + 1):
+            G, odd = divmod(k - 3, 2)
+            if k + 2 < PAIRS:
+                load_flows(k + 2)
+            if k == 3:
+                for g in range(NG):
+                    load_grad(1, g)
+            if k < PAIRS:
+                trs(k, 0)
+                trs(k, 1)
+            dts_now = [0, 1] if k == 3 else [k - 2]
+            for j in dts_now:
+                dt(j)
+                dt_copy(j)
+            if odd == 1:
+                dx(G)
+                dx_out(G)
+            for s in range(2):
+                for g in range(NG):
+                    mm(k - 1, s, g)
+                dxw(k - 1, s)
+            if k == 3:
+                w_q()
+            tok(G, odd)
+            for s in range(2):
+                if k + 1 < PAIRS:
+                    sort_words(k + 1, s)
+                if k < PAIRS:
+                    quant(k, s)
+                if gz1:
+                    gz1.pop(0)()
+            for j in dts_now:
+                dt_q(j)
+            if odd == 1:
+                tok_q(G)
+            if gz1:
+                gz1.pop(0)()
+            if 8 <= k < 16:
+                x_int(*divmod(k - 8, 4))
+            if k == 16:
+                x_q()
+        G = GROUPS - 1
+        dt(15, (0,))
+        for j in range(3):
+            dw(j)
+        dt_copy(15, slice(0, 1))
+        dt_q(15, 0, 1)
+        tok(G, 0)
+        dt(15, (1,))
+        for j in range(3, 5):
+            dw(j)
+        dt_copy(15, slice(1, 2))
+        dt_q(15, 1, 2)
+        dx(G)
+        dx_out(G)
+        for j in range(5, 7):
+            dw(j)
+        tok(G, 1)
+        tok_q(G)
+        dw(G)
+        dw_out()

@@ -29,8 +29,8 @@ def tile_encoder_flows_pb_v_kernel(tc, flows, x_gcn1, W2, b2, dinv, grad_out, ou
     with ExitStack() as ctx:
         keep = ctx.enter_context(tc.tile_pool(name="keep", bufs=1))
         work = ctx.enter_context(tc.tile_pool(name="work", bufs=2))
-        tpool = ctx.enter_context(tc.psum_pool(name="tpool", bufs=4))
-        apool = ctx.enter_context(tc.psum_pool(name="apool", bufs=4))
+        tpool = ctx.enter_context(tc.psum_pool(name="tpool", bufs=5))
+        apool = ctx.enter_context(tc.psum_pool(name="apool", bufs=3))
         ctx.enter_context(tc.manual_schedule())
 
         ident = keep.tile([P, P], F32, name="ident", align_bytes=64)
@@ -59,9 +59,12 @@ def tile_encoder_flows_pb_v_kernel(tc, flows, x_gcn1, W2, b2, dinv, grad_out, ou
             else:
                 nc.sync.dma_start(out=raw[k][:, s, :], in_=src[:, 2 * h + s, :])
 
-        def load_grad(b, g):
+        def load_grad(b, g, parts=1):
             gr[b, g] = work.tile([P, 4, I], BF16, name="gr", bufs=4, align_bytes=64)
-            nc.sync.dma_start(out=gr[b, g][:], in_=grad_out[b, 512 * g:512 * (g + 1), :].rearrange("(p j) w -> p j w", j=4))
+            src = grad_out[b, 512 * g:512 * (g + 1), :].rearrange("(p j) w -> p j w", j=4)
+            n = 4 // parts
+            for i in range(parts):
+                nc.sync.dma_start(out=gr[b, g][:, n * i:n * (i + 1), :], in_=src[:, n * i:n * (i + 1), :])
 
         def load_w():
             misc["w"] = keep.tile([P, I], BF16, name="wraw", align_bytes=64)
@@ -82,8 +85,8 @@ def tile_encoder_flows_pb_v_kernel(tc, flows, x_gcn1, W2, b2, dinv, grad_out, ou
         def gz_int(b, g, u, eng="v"):
             if (b, g) not in gi:
                 gi[b, g] = work.tile([P, 4 * I], BF16, name="gi", bufs=2, align_bytes=64)
-            out = gi[b, g][:, 1024 * u:1024 * (u + 1)].rearrange("p (m e j) -> p m e j", e=2, j=4)
-            src = gm[b, g][:].rearrange("p j (m u e) -> p u m e j", u=2, e=2)[:, u]
+            out = gi[b, g][:, 1024 * u:1024 * (u + 1)].rearrange("p (m e j) -> p m j e", e=2, j=4)
+            src = gm[b, g][:].rearrange("p j (m u e) -> p u m j e", u=2, e=2)[:, u]
             if eng == "v":
                 nc.vector.tensor_copy(out=out, in_=src)
             else:
@@ -173,10 +176,12 @@ def tile_encoder_flows_pb_v_kernel(tc, flows, x_gcn1, W2, b2, dinv, grad_out, ou
                 dts[k] = work.tile([P, 256], U8, name="dts", bufs=4, align_bytes=64)
             nc.vector.quantize_mx(out=dtc[k][:, P * a:P * z].bitcast(E5), scales=dts[k][:, P * a:P * z], in_=dtb[k][:, 512 * a:512 * z])
 
-        def dx(G):
-            ps = apool.tile([P, I], F32, name="acc")
-            acc["dx", G] = ps
-            for t in range(4):
+        def dx(G, ts=(0, 1, 2, 3)):
+            if ("dx", G) not in acc:
+                ps = apool.tile([P, I], F32, name="acc")
+                acc["dx", G] = ps
+            ps = acc["dx", G]
+            for t in ts:
                 k, s = 2 * G + t // 2, t % 2
                 cols = slice(P * s, P * (s + 1))
                 win = slice(384 - P * t, 896 - P * t)
@@ -196,8 +201,8 @@ def tile_encoder_flows_pb_v_kernel(tc, flows, x_gcn1, W2, b2, dinv, grad_out, ou
         def tok(G, h, eng="v"):
             if G not in DI:
                 DI[G] = work.tile([P, 4 * I], BF16, name="DI", bufs=2, align_bytes=64)
-            out = DI[G][:, 1024 * h:1024 * (h + 1)].rearrange("p (n t) -> p n t", t=4)
-            src = D[G][:, :, 256 * h:256 * (h + 1)].rearrange("p t n -> p n t")
+            out = DI[G][:, 1024 * h:1024 * (h + 1)].rearrange("p (c i t) -> p c t i", i=4, t=4)
+            src = D[G][:, :, 256 * h:256 * (h + 1)].rearrange("p t (c i) -> p c t i", i=4)
             if eng == "v":
                 nc.vector.tensor_copy(out=out, in_=src)
             else:
@@ -211,7 +216,9 @@ def tile_encoder_flows_pb_v_kernel(tc, flows, x_gcn1, W2, b2, dinv, grad_out, ou
         def x_int(b, part):
             if "xi" not in misc:
                 misc["xi"] = keep.tile([P, GROUPS, R, 4], BF16, name="xi", align_bytes=64)
-            nc.vector.tensor_copy(out=misc["xi"][:, 4 * b + part:4 * b + part + 1], in_=misc["x"][:, 4 * b + part:4 * b + part + 1].rearrange("p g t w -> p g w t"))
+            g = 4 * b + part
+            nc.vector.tensor_copy(out=misc["xi"][:, g].rearrange("p (c i) t -> p c t i", i=4),
+                                  in_=misc["x"][:, g].rearrange("p t (c i) -> p c t i", i=4))
 
         def x_q():
             misc["xc"] = keep.tile([P, GROUPS * R], U32, name="xc", align_bytes=64)
@@ -226,7 +233,7 @@ def tile_encoder_flows_pb_v_kernel(tc, flows, x_gcn1, W2, b2, dinv, grad_out, ou
                                 rhs=tcod[G][:].bitcast(E5), rhs_scale=tscl[G][:], start=(G == 0), stop=(G == GROUPS - 1))
 
         def dw_out():
-            wo = work.tile([P, I], F32, name="ob", bufs=2, align_bytes=64)
+            wo = work.tile([P, I], F32, name="wo", bufs=1, align_bytes=64)
             nc.vector.tensor_copy(out=wo[:].rearrange("p (m u e) -> p m u e", u=2, e=2),
                                   in_=acc["dw"][:].rearrange("p (u m e) -> p m u e", u=2, e=2))
             nc.sync.dma_start(out=out_1, in_=wo[:])
@@ -247,13 +254,14 @@ def tile_encoder_flows_pb_v_kernel(tc, flows, x_gcn1, W2, b2, dinv, grad_out, ou
             nc.vector.quantize_mx(out=wcodes[:, 384:512].bitcast(E4), scales=wscale[:, 384:512], in_=misc["wi"][:])
 
         load_dv()
-        load_grad(0, 0)
+        load_grad(0, 0, 2)
         load_flows(0, 0)
         load_grad(0, 1)
         load_flows(0, 1)
         load_grad(0, 2)
+        load_flows(1, 0)
         load_grad(0, 3)
-        load_flows(1)
+        load_flows(1, 1)
         load_flows(2)
         load_w()
         load_flows(3)
@@ -276,38 +284,39 @@ def tile_encoder_flows_pb_v_kernel(tc, flows, x_gcn1, W2, b2, dinv, grad_out, ou
         trs(0, 0)
         gz_mul(0, 1)
         gz_q(0, 0)
-        trs(0, 1)
         gz_int(0, 1, 0)
         gz_int(0, 1, 1, "s")
         quant(0, 0)
+        trs(0, 1)
         gz_mul(0, 2)
-        gz_mul(0, 3)
-        gz_int(0, 2, 0, "s")
-        gz_int(0, 2, 1)
         gz_q(0, 1)
+        mms([(0, 0)], (0, 1))
+        gz_int(0, 2, 0)
+        gz_int(0, 2, 1, "s")
         quant(0, 1)
-        gz_int(0, 3, 0)
+        gz_mul(0, 3)
         gz_q(0, 2)
-        gz_int(0, 3, 1)
-        mms([(0, 0), (0, 1)], (0, 1))
         trs(1, 0)
-        trs(1, 1)
+        mms([(0, 1)], (0, 1))
         mms([(0, 0), (0, 1)], (2,))
+        gz_int(0, 3, 0)
+        trs(1, 1)
+        gz_int(0, 3, 1)
+        quant(1, 0)
         gz_q(0, 3)
         mms([(0, 0), (0, 1)], (3,))
-        quant(1, 0)
-        sort_words(3, 0)
         quant(1, 1)
         dxw(0, 0)
         dxw(0, 1)
         trs(2, 0)
-        trs(2, 1)
-        sort_words(3, 1)
+        sort_words(3, 0)
         mms([(1, 0)], range(4))
-        mms([(1, 1)], range(4))
-        quant(2, 0)
-        quant(2, 1)
         dxw(1, 0)
+        trs(2, 1)
+        quant(2, 0)
+        sort_words(3, 1)
+        mms([(1, 1)], range(4))
+        quant(2, 1)
         dxw(1, 1)
         w_tr()
         w_copy()
@@ -315,16 +324,15 @@ def tile_encoder_flows_pb_v_kernel(tc, flows, x_gcn1, W2, b2, dinv, grad_out, ou
         gz1 = []
         for g in range(NG):
             gz1 += [lambda g=g: gz_mul(1, g), lambda g=g: gz_int(1, g, 0), lambda g=g: gz_int(1, g, 1), lambda g=g: gz_q(1, g)]
-        for k in range(3, PAIRS + 1):
+        for k in range(3, PAIRS):
             G, odd = divmod(k - 3, 2)
             if k + 2 < PAIRS:
                 load_flows(k + 2)
             if k == 3:
                 for g in range(NG):
                     load_grad(1, g)
-            if k < PAIRS:
-                trs(k, 0)
-                trs(k, 1)
+            trs(k, 0)
+            trs(k, 1)
             dts_now = [0, 1] if k == 3 else [k - 2]
             for j in dts_now:
                 dt(j)
@@ -342,8 +350,7 @@ def tile_encoder_flows_pb_v_kernel(tc, flows, x_gcn1, W2, b2, dinv, grad_out, ou
             for s in range(2):
                 if k + 1 < PAIRS:
                     sort_words(k + 1, s)
-                if k < PAIRS:
-                    quant(k, s)
+                quant(k, s)
                 if gz1:
                     gz1.pop(0)()
             for j in dts_now:
@@ -354,25 +361,30 @@ def tile_encoder_flows_pb_v_kernel(tc, flows, x_gcn1, W2, b2, dinv, grad_out, ou
                 gz1.pop(0)()
             if 8 <= k < 16:
                 x_int(*divmod(k - 8, 4))
-            if k == 16:
-                x_q()
         G = GROUPS - 1
+        tok(G - 1, 1)
+        for s in range(2):
+            for g in range(NG):
+                mm(15, s, g)
+            dxw(15, s)
+        x_q()
+        tok_q(G - 1)
+        dt(14)
+        dt_copy(14)
         dt(15, (0,))
-        for j in range(3):
+        for j in range(2):
             dw(j)
-        dt_copy(15, slice(0, 1))
-        dt_q(15, 0, 1)
-        tok(G, 0)
         dt(15, (1,))
-        for j in range(3, 5):
-            dw(j)
-        dt_copy(15, slice(1, 2))
-        dt_q(15, 1, 2)
+        dt_copy(15)
+        tok(G, 0)
+        dt_q(14)
+        tok(G, 1)
+        dx(G - 1)
+        dx_out(G - 1)
+        dt_q(15)
+        tok_q(G)
         dx(G)
         dx_out(G)
-        for j in range(5, 7):
+        for j in range(2, GROUPS):
             dw(j)
-        tok(G, 1)
-        tok_q(G)
-        dw(G)
         dw_out()

@@ -21,7 +21,7 @@ GROUPS = B * N // 512
 
 FLOPS = 2 * B * N * N * I + 2 * 2 * B * N * I * R
 
-PERM = {(k, s) for k in range(3, PAIRS) for s in range(2)} - {(6, 1), (8, 0), (8, 1)}
+SORTED = set(range(2, PAIRS)) - {6}
 
 
 def tile_encoder_flows_pb_v_kernel(tc, flows, x_gcn1, W2, b2, dinv, grad_out, out_0, out_1):
@@ -36,21 +36,19 @@ def tile_encoder_flows_pb_v_kernel(tc, flows, x_gcn1, W2, b2, dinv, grad_out, ou
         ident = keep.tile([P, P], F32, name="ident", align_bytes=64)
         make_identity(nc, ident[:])
         dv = keep.tile([P, GROUPS, 4], F32, name="dv", align_bytes=64)
-        wcodes = keep.tile([P, 896], U32, name="wcodes", align_bytes=64)
-        wscale = keep.tile([P, 896], U8, name="wscale", align_bytes=64)
-        nc.gpsimd.memset(wcodes[:].bitcast(I32), 0)
-        nc.gpsimd.memset(wscale[:].bitcast(I32), 0)
+        wcodes = keep.tile([P, R], U32, name="wcodes", align_bytes=64)
+        wscale = keep.tile([P, R], U8, name="wscale", align_bytes=64)
 
         raw, perm, ft, fc, fs, gr, gm, gi, gc, gs = {}, {}, {}, {}, {}, {}, {}, {}, {}, {}
         bank, acc, D, dtb, dtbank, dtc, dts, DI, tcod, tscl = {}, {}, {}, {}, {}, {}, {}, {}, {}, {}
-        misc = {}
+        misc, xt, dxbank, xi = {}, {}, {}, {}
 
         def load_dv():
             nc.scalar.dma_start(out=dv[:], in_=dinv.rearrange("b (g p t) -> p (b g) t", p=P, t=4))
 
         def load_flows(k, s=None):
             if k not in raw:
-                raw[k] = work.tile([P, 2, N], BF16, name="raw", bufs=6, align_bytes=64)
+                raw[k] = work.tile([P, 2, N], BF16, name="raw", bufs=5, align_bytes=64)
             b, rest = divmod(k, PAIRS // B)
             g, h = divmod(rest, 2)
             src = flows[b, 512 * g:512 * (g + 1), :].rearrange("(p t) c -> p t c", t=4)
@@ -71,7 +69,7 @@ def tile_encoder_flows_pb_v_kernel(tc, flows, x_gcn1, W2, b2, dinv, grad_out, ou
             nc.sync.dma_start(out=misc["w"][:], in_=W2)
 
         def load_x():
-            misc["x"] = keep.tile([P, GROUPS, 4, R], BF16, name="xraw", align_bytes=64)
+            misc["x"] = work.tile([P, GROUPS, 4, R], BF16, name="x", tag="raw", bufs=5, align_bytes=64)
             for b in range(B):
                 nc.sync.dma_start(out=misc["x"][:, 4 * b:4 * b + 4], in_=x_gcn1[b].rearrange("(g p t) w -> p g t w", p=P, t=4))
 
@@ -81,6 +79,11 @@ def tile_encoder_flows_pb_v_kernel(tc, flows, x_gcn1, W2, b2, dinv, grad_out, ou
             for j in js:
                 nc.vector.tensor_scalar(out=gm[b, g][:, j, :], in0=gr[b, g][:, j, :],
                                         scalar1=dv[:, 4 * b + g, j:j + 1], scalar2=None, op0=MULT)
+
+        def gz_int_all(b, g):
+            gi[b, g] = work.tile([P, 4 * I], BF16, name="gi", bufs=2, align_bytes=64)
+            nc.vector.tensor_copy(out=gi[b, g][:].rearrange("p (u m e j) -> p u m j e", u=2, e=2, j=4),
+                                  in_=gm[b, g][:].rearrange("p j (m u e) -> p u m j e", u=2, e=2))
 
         def gz_int(b, g, u, eng="v"):
             if (b, g) not in gi:
@@ -97,11 +100,11 @@ def tile_encoder_flows_pb_v_kernel(tc, flows, x_gcn1, W2, b2, dinv, grad_out, ou
             gs[b, g] = keep.tile([P, I], U8, name="gs%d%d" % (b, g), align_bytes=64)
             nc.vector.quantize_mx(out=gc[b, g][:].bitcast(E5), scales=gs[b, g][:], in_=gi[b, g][:])
 
-        def sort_words(k, s):
-            if (k, s) in PERM:
-                perm[k, s] = work.tile([P, NG, 2, P], F32, name="perm", bufs=3, align_bytes=64)
-                nc.vector.tensor_copy(out=perm[k, s][:],
-                                      in_=raw[k][:, s, :].bitcast(F32).rearrange("p (g m u) -> p g u m", g=NG, u=2))
+        def sort_words(k):
+            if k in SORTED:
+                perm[k] = work.tile([P, 2 * NG, 2, P], F32, name="perm", bufs=2, align_bytes=64)
+                words = raw[k][:].rearrange("p v c -> p (v c)").bitcast(F32)
+                nc.vector.tensor_copy(out=perm[k][:], in_=words.rearrange("p (g m u) -> p g u m", m=P, u=2))
 
         def tr(k, s, h):
             ps = tpool.tile([P, 4, P], F32, name="ps")
@@ -109,39 +112,41 @@ def tile_encoder_flows_pb_v_kernel(tc, flows, x_gcn1, W2, b2, dinv, grad_out, ou
             words = raw[k][:, s, :].bitcast(F32)
             for q in range(4):
                 g, u = 2 * h + q // 2, q % 2
-                if (k, s) in PERM:
-                    src = perm[k, s][:, g, u, :]
+                if k in SORTED:
+                    src = perm[k][:, NG * s + g, u, :]
                 else:
                     src = words[:, 256 * g + u:256 * (g + 1):2]
                 nc.tensor.transpose(ps[:, q, :], src, ident[:])
 
         def tr_copy(k, s, h, eng="s"):
-            if (k, s) not in ft:
-                ft[k, s] = work.tile([P, 4 * NG * P], BF16, name="ft", bufs=5, align_bytes=64)
-            out = ft[k, s][:].bitcast(F32)[:, 512 * h:512 * (h + 1)].rearrange("p (g r u) -> p g r u", g=2, u=2)
+            if k not in ft:
+                ft[k] = work.tile([P, 8 * NG * P], BF16, name="ft", bufs=3, align_bytes=64)
+            w0 = 1024 * s + 512 * h
+            out = ft[k][:].bitcast(F32)[:, w0:w0 + 512].rearrange("p (g r u) -> p g r u", g=2, u=2)
             src = bank[k, s, h][:].rearrange("p (g u) r -> p g r u", u=2)
             if eng == "s":
                 nc.scalar.copy(out=out, in_=src)
             else:
                 nc.vector.tensor_copy(out=out, in_=src)
 
-        def quant(k, s):
-            fc[k, s] = work.tile([P, NG * P], U32, name="fc", bufs=6, align_bytes=64)
-            fs[k, s] = work.tile([P, NG * P], U8, name="fs", bufs=6, align_bytes=64)
-            nc.vector.quantize_mx(out=fc[k, s][:].bitcast(E4), scales=fs[k, s][:], in_=ft[k, s][:])
+        def quant(k, a=0, z=2):
+            if k not in fc:
+                fc[k] = work.tile([P, 2 * NG * P], U32, name="fc", bufs=3, align_bytes=64)
+                fs[k] = work.tile([P, 2 * NG * P], U8, name="fs", bufs=3, align_bytes=64)
+            nc.vector.quantize_mx(out=fc[k][:, 512 * a:512 * z].bitcast(E4), scales=fs[k][:, 512 * a:512 * z], in_=ft[k][:, 2048 * a:2048 * z])
 
         def mm(k, s, g):
             b = k // (PAIRS // B)
             if g == 0:
                 acc[k, s] = apool.tile([P, I], F32, name="acc")
-            cols = slice(P * g, P * (g + 1))
-            nc.tensor.matmul_mx(out=acc[k, s][:], lhsT=fc[k, s][:, cols].bitcast(E4), lhsT_scale=fs[k, s][:, cols],
+            cols = slice(512 * s + P * g, 512 * s + P * (g + 1))
+            nc.tensor.matmul_mx(out=acc[k, s][:], lhsT=fc[k][:, cols].bitcast(E4), lhsT_scale=fs[k][:, cols],
                                 rhs=gc[b, g][:].bitcast(E5), rhs_scale=gs[b, g][:], start=(g == 0), stop=(g == NG - 1))
 
         def dxw(k, s, eng="s", half=None):
             G, t = divmod(2 * k + s, 4)
             if G not in D:
-                D[G] = work.tile([P, 4, I], BF16, name="D", bufs=3, align_bytes=64)
+                D[G] = work.tile([P, 4, I], BF16, name="D", bufs=4, align_bytes=64)
             cols = slice(0, I) if half is None else slice(256 * half, 256 * (half + 1))
             if eng == "s":
                 nc.scalar.activation(out=D[G][:, t, cols], in_=acc[k, s][:, cols], func=COPY, scale=dv[:, G, t:t + 1])
@@ -161,42 +166,52 @@ def tile_encoder_flows_pb_v_kernel(tc, flows, x_gcn1, W2, b2, dinv, grad_out, ou
                     nc.tensor.transpose(ps[:, 2 * s + u, :], words[:, P * u:P * (u + 1)], ident[:])
 
         def dt_copy(k, slots=slice(0, 2), eng="s"):
-            if k not in dtb:
-                dtb[k] = work.tile([P, 1024], BF16, name="dtb", bufs=3, align_bytes=64)
-            out = dtb[k][:].bitcast(F32).rearrange("p (v r u) -> p v r u", v=2, u=2)[:, slots]
+            G, h = divmod(k, 2)
+            if G not in dtb:
+                dtb[G] = work.tile([P, 2048], BF16, name="dtb", bufs=2, align_bytes=64)
+            out = dtb[G][:].bitcast(F32)[:, 512 * h:512 * (h + 1)].rearrange("p (v r u) -> p v r u", v=2, u=2)[:, slots]
             src = dtbank[k][:].rearrange("p (v u) r -> p v r u", u=2)[:, slots]
             if eng == "s":
                 nc.scalar.copy(out=out, in_=src)
             else:
                 nc.vector.tensor_copy(out=out, in_=src)
 
-        def dt_q(k, a=0, z=2):
-            if k not in dtc:
-                dtc[k] = work.tile([P, 256], U32, name="dtc", bufs=4, align_bytes=64)
-                dts[k] = work.tile([P, 256], U8, name="dts", bufs=4, align_bytes=64)
-            nc.vector.quantize_mx(out=dtc[k][:, P * a:P * z].bitcast(E5), scales=dts[k][:, P * a:P * z], in_=dtb[k][:, 512 * a:512 * z])
+        def dt_q(G, a=0, z=2):
+            if G not in dtc:
+                dtc[G] = work.tile([P, 512], U32, name="dtc", bufs=2, align_bytes=64)
+                dts[G] = work.tile([P, 512], U8, name="dts", bufs=2, align_bytes=64)
+            cols = slice(256 * a, 256 * z)
+            nc.vector.quantize_mx(out=dtc[G][:, cols].bitcast(E5), scales=dts[G][:, cols], in_=dtb[G][:, 1024 * a:1024 * z])
 
-        def dx(G, ts=(0, 1, 2, 3)):
-            if ("dx", G) not in acc:
-                ps = apool.tile([P, I], F32, name="acc")
-                acc["dx", G] = ps
-            ps = acc["dx", G]
-            for t in ts:
-                k, s = 2 * G + t // 2, t % 2
-                cols = slice(P * s, P * (s + 1))
-                win = slice(384 - P * t, 896 - P * t)
-                nc.tensor.matmul_mx(out=ps[:], lhsT=dtc[k][:, cols].bitcast(E5), lhsT_scale=dts[k][:, cols],
-                                    rhs=wcodes[:, win].bitcast(E4), rhs_scale=wscale[:, win], start=(t == 0), stop=(t == 3))
+        def dx(G):
+            acc["dx", G] = apool.tile([P, I], F32, name="acc")
+            nc.tensor.matmul_mx(out=acc["dx", G][:], lhsT=wcodes[:].bitcast(E4), lhsT_scale=wscale[:],
+                                rhs=dtc[G][:].bitcast(E5), rhs_scale=dts[G][:], start=True, stop=True)
+
+        def dx_copy(G):
+            xt[G] = work.tile([P, I], F32, name="xt", bufs=2, align_bytes=64)
+            nc.scalar.copy(out=xt[G][:], in_=acc["dx", G][:])
+
+        def dx_tr(G):
+            ps = tpool.tile([P, 4, P], F32, name="ps")
+            dxbank[G] = ps
+            for t in range(4):
+                nc.tensor.transpose(ps[:, t, :], xt[G][:, P * t:P * (t + 1)], ident[:])
 
         def dx_out(G, eng="s"):
-            ob = work.tile([P, I], F32, name="ob", bufs=2, align_bytes=64)
+            ob = work.tile([P, 4, R], F32, name="ob", bufs=2, align_bytes=64)
             if eng == "s":
-                nc.scalar.copy(out=ob[:], in_=acc["dx", G][:])
+                nc.scalar.copy(out=ob[:], in_=dxbank[G][:])
             else:
-                nc.vector.tensor_copy(out=ob[:], in_=acc["dx", G][:])
+                nc.vector.tensor_copy(out=ob[:], in_=dxbank[G][:])
             b, g = divmod(G, GROUPS // B)
             dst = out_0[b, 512 * g:512 * (g + 1), :].rearrange("(p t) w -> p t w", t=4)
-            nc.sync.dma_start(out=dst, in_=ob[:].rearrange("p (t w) -> p t w", t=4))
+            nc.sync.dma_start(out=dst, in_=ob[:])
+
+        def tok_all(G):
+            DI[G] = work.tile([P, 4 * I], BF16, name="DI", bufs=2, align_bytes=64)
+            nc.vector.tensor_copy(out=DI[G][:].rearrange("p (c i t) -> p c t i", i=4, t=4),
+                                  in_=D[G][:].rearrange("p t (c i) -> p c t i", i=4))
 
         def tok(G, h, eng="v"):
             if G not in DI:
@@ -213,17 +228,20 @@ def tile_encoder_flows_pb_v_kernel(tc, flows, x_gcn1, W2, b2, dinv, grad_out, ou
             tscl[G] = keep.tile([P, I], U8, name="ts%d" % G, align_bytes=64)
             nc.vector.quantize_mx(out=tcod[G][:].bitcast(E5), scales=tscl[G][:], in_=DI[G][:])
 
-        def x_int(b, part):
-            if "xi" not in misc:
-                misc["xi"] = keep.tile([P, GROUPS, R, 4], BF16, name="xi", align_bytes=64)
-            g = 4 * b + part
-            nc.vector.tensor_copy(out=misc["xi"][:, g].rearrange("p (c i) t -> p c t i", i=4),
-                                  in_=misc["x"][:, g].rearrange("p t (c i) -> p c t i", i=4))
+        def x_int(i):
+            b = i // 2
+            if b not in xi:
+                xi[b] = work.tile([P, 4, R, 4], BF16, name="xi", tag="gi", bufs=2, align_bytes=64)
+            for g in range(2):
+                src = misc["x"][:, 2 * i + g].rearrange("p t (c i) -> p c t i", i=4)
+                nc.vector.tensor_copy(out=xi[b][:, 2 * (i % 2) + g].rearrange("p (c i) t -> p c t i", i=4), in_=src)
 
-        def x_q():
-            misc["xc"] = keep.tile([P, GROUPS * R], U32, name="xc", align_bytes=64)
-            misc["xs"] = keep.tile([P, GROUPS * R], U8, name="xs", align_bytes=64)
-            nc.vector.quantize_mx(out=misc["xc"][:].bitcast(E4), scales=misc["xs"][:], in_=misc["xi"][:].rearrange("p g w t -> p (g w t)"))
+        def x_q(b):
+            if b == 0:
+                misc["xc"] = keep.tile([P, GROUPS * R], U32, name="xc", align_bytes=64)
+                misc["xs"] = keep.tile([P, GROUPS * R], U8, name="xs", align_bytes=64)
+            cols = slice(512 * b, 512 * (b + 1))
+            nc.vector.quantize_mx(out=misc["xc"][:, cols].bitcast(E4), scales=misc["xs"][:, cols], in_=xi[b][:].rearrange("p g w t -> p (g w t)"))
 
         def dw(G):
             if G == 0:
@@ -251,7 +269,7 @@ def tile_encoder_flows_pb_v_kernel(tc, flows, x_gcn1, W2, b2, dinv, grad_out, ou
                            in_=misc["wps"][:, 0:2, :].rearrange("p u r -> p r u"))
 
         def w_q():
-            nc.vector.quantize_mx(out=wcodes[:, 384:512].bitcast(E4), scales=wscale[:, 384:512], in_=misc["wi"][:])
+            nc.vector.quantize_mx(out=wcodes[:].bitcast(E4), scales=wscale[:], in_=misc["wi"][:])
 
         load_dv()
         load_grad(0, 0, 2)
@@ -266,7 +284,6 @@ def tile_encoder_flows_pb_v_kernel(tc, flows, x_gcn1, W2, b2, dinv, grad_out, ou
         load_w()
         load_flows(3)
         load_flows(4)
-        load_x()
 
         def trs(k, s):
             for h in range(2):
@@ -280,54 +297,68 @@ def tile_encoder_flows_pb_v_kernel(tc, flows, x_gcn1, W2, b2, dinv, grad_out, ou
 
         gz_mul(0, 0)
         gz_int(0, 0, 0)
-        gz_int(0, 0, 1)
+        gz_int(0, 0, 1, "s")
         trs(0, 0)
         gz_mul(0, 1)
         gz_q(0, 0)
         gz_int(0, 1, 0)
         gz_int(0, 1, 1, "s")
-        quant(0, 0)
+        quant(0, 0, 1)
         trs(0, 1)
         gz_mul(0, 2)
         gz_q(0, 1)
         mms([(0, 0)], (0, 1))
         gz_int(0, 2, 0)
         gz_int(0, 2, 1, "s")
-        quant(0, 1)
+        quant(0, 1, 2)
         gz_mul(0, 3)
         gz_q(0, 2)
         trs(1, 0)
         mms([(0, 1)], (0, 1))
-        mms([(0, 0), (0, 1)], (2,))
         gz_int(0, 3, 0)
+        gz_int(0, 3, 1, "s")
         trs(1, 1)
-        gz_int(0, 3, 1)
-        quant(1, 0)
+        mms([(0, 0), (0, 1)], (2,))
+        quant(1, 0, 1)
         gz_q(0, 3)
+        sort_words(2)
         mms([(0, 0), (0, 1)], (3,))
-        quant(1, 1)
-        dxw(0, 0)
-        dxw(0, 1)
-        trs(2, 0)
-        sort_words(3, 0)
+        quant(1, 1, 2)
         mms([(1, 0)], range(4))
-        dxw(1, 0)
+        trs(2, 0)
+        dxw(0, 0, "v")
+        dxw(0, 1, "v")
         trs(2, 1)
-        quant(2, 0)
-        sort_words(3, 1)
+        dxw(1, 0)
+        sort_words(3)
         mms([(1, 1)], range(4))
-        quant(2, 1)
-        dxw(1, 1)
         w_tr()
         w_copy()
+        quant(2)
+        dxw(1, 1)
 
-        gz1 = []
-        for g in range(NG):
-            gz1 += [lambda g=g: gz_mul(1, g), lambda g=g: gz_int(1, g, 0), lambda g=g: gz_int(1, g, 1), lambda g=g: gz_q(1, g)]
+        load_flows(5)
+        plan = {
+            3: ["sort", "quant", (gz_mul, 1, 0), (dt_q, 0), (gz_int_all, 1, 0)],
+            4: ["sort", (gz_mul, 1, 1), (gz_q, 1, 0), "quant", (tok_all, 0)],
+            5: ["sort", (gz_int_all, 1, 1), "quant", (dt_q, 1), (tok_q, 0)],
+            6: ["sort", (gz_mul, 1, 2), (gz_q, 1, 1), "quant", (gz_int_all, 1, 2), (gz_mul, 1, 3)],
+            7: ["sort", (gz_q, 1, 2), "quant", (dt_q, 2), (gz_int_all, 1, 3)],
+            8: ["sort", (gz_q, 1, 3), "quant", (tok_all, 1)],
+            9: ["sort", (tok_q, 1), "quant", (dt_q, 3), (tok_all, 2)],
+            10: ["sort", (tok_q, 2), "quant", (tok_all, 3)],
+            11: ["sort", (tok_q, 3), "quant", (dt_q, 4)],
+            12: [(tok_all, 4), "sort", "quant", (tok_q, 4)],
+            13: ["sort", (x_int, 0), "quant", (dt_q, 5), (x_int, 1)],
+            14: [(tok_all, 5), "sort", (x_q, 0), "quant", (tok_q, 5)],
+            15: [(x_int, 2), (x_int, 3), "quant", (x_q, 1), (dt_q, 6)],
+        }
         for k in range(3, PAIRS):
             G, odd = divmod(k - 3, 2)
-            if k + 2 < PAIRS:
-                load_flows(k + 2)
+            if k + 3 < PAIRS:
+                load_flows(k + 3)
+            elif k + 3 == PAIRS:
+                load_x()
             if k == 3:
                 for g in range(NG):
                     load_grad(1, g)
@@ -337,54 +368,56 @@ def tile_encoder_flows_pb_v_kernel(tc, flows, x_gcn1, W2, b2, dinv, grad_out, ou
             for j in dts_now:
                 dt(j)
                 dt_copy(j)
+            if odd == 0 and G > 0:
+                dx_tr(G - 1)
+                dx_out(G - 1)
             if odd == 1:
                 dx(G)
-                dx_out(G)
+                dx_copy(G)
             for s in range(2):
                 for g in range(NG):
                     mm(k - 1, s, g)
                 dxw(k - 1, s)
             if k == 3:
                 w_q()
-            tok(G, odd)
-            for s in range(2):
-                if k + 1 < PAIRS:
-                    sort_words(k + 1, s)
-                quant(k, s)
-                if gz1:
-                    gz1.pop(0)()
-            for j in dts_now:
-                dt_q(j)
-            if odd == 1:
-                tok_q(G)
-            if gz1:
-                gz1.pop(0)()
-            if 8 <= k < 16:
-                x_int(*divmod(k - 8, 4))
+            for item in plan[k]:
+                if item == "sort":
+                    if k + 1 < PAIRS:
+                        sort_words(k + 1)
+                elif item == "quant":
+                    quant(k)
+                else:
+                    item[0](*item[1:])
         G = GROUPS - 1
-        tok(G - 1, 1)
         for s in range(2):
             for g in range(NG):
                 mm(15, s, g)
             dxw(15, s)
-        x_q()
-        tok_q(G - 1)
+        tok_all(G - 1)
         dt(14)
         dt_copy(14)
         dt(15, (0,))
-        for j in range(2):
-            dw(j)
+        dx(G - 1)
+        dx_copy(G - 1)
         dt(15, (1,))
         dt_copy(15)
-        tok(G, 0)
-        dt_q(14)
-        tok(G, 1)
-        dx(G - 1)
+        dw(0)
+        dw(1)
+        dx_tr(G - 1)
         dx_out(G - 1)
-        dt_q(15)
-        tok_q(G)
+        dt_q(G, 0, 1)
+        tok(G, 0)
+        dt_q(G, 1, 2)
+        tok_q(G - 1)
+        tok(G, 1)
+        dw(2)
+        dw(3)
         dx(G)
-        dx_out(G)
-        for j in range(2, GROUPS):
+        dx_copy(G)
+        tok_q(G)
+        for j in range(4, GROUPS - 1):
             dw(j)
+        dx_tr(G)
+        dx_out(G)
+        dw(G)
         dw_out()

@@ -21,7 +21,8 @@ GROUPS = B * N // 512
 
 FLOPS = 2 * B * N * N * I + 2 * 2 * B * N * I * R
 
-SORTED = set(range(2, PAIRS)) - {6}
+HALF = ()
+SORTED = {k: 1 if k in HALF else 2 for k in range(2, PAIRS)}
 
 
 def tile_encoder_flows_pb_v_kernel(tc, flows, x_gcn1, W2, b2, dinv, grad_out, out_0, out_1):
@@ -101,10 +102,10 @@ def tile_encoder_flows_pb_v_kernel(tc, flows, x_gcn1, W2, b2, dinv, grad_out, ou
             nc.vector.quantize_mx(out=gc[b, g][:].bitcast(E5), scales=gs[b, g][:], in_=gi[b, g][:])
 
         def sort_words(k):
-            if k in SORTED:
-                perm[k] = work.tile([P, 2 * NG, 2, P], F32, name="perm", bufs=2, align_bytes=64)
-                words = raw[k][:].rearrange("p v c -> p (v c)").bitcast(F32)
-                nc.vector.tensor_copy(out=perm[k][:], in_=words.rearrange("p (g m u) -> p g u m", m=P, u=2))
+            n = SORTED.get(k, 0)
+            perm[k] = work.tile([P, 2 * NG, 2, P], F32, name="perm", bufs=2, align_bytes=64)
+            words = raw[k][:, 0:n, :].rearrange("p v c -> p (v c)").bitcast(F32)
+            nc.vector.tensor_copy(out=perm[k][:, 0:NG * n], in_=words.rearrange("p (g m u) -> p g u m", m=P, u=2))
 
         def tr(k, s, h):
             ps = tpool.tile([P, 4, P], F32, name="ps")
@@ -112,7 +113,7 @@ def tile_encoder_flows_pb_v_kernel(tc, flows, x_gcn1, W2, b2, dinv, grad_out, ou
             words = raw[k][:, s, :].bitcast(F32)
             for q in range(4):
                 g, u = 2 * h + q // 2, q % 2
-                if k in SORTED:
+                if s < SORTED.get(k, 0):
                     src = perm[k][:, NG * s + g, u, :]
                 else:
                     src = words[:, 256 * g + u:256 * (g + 1):2]
@@ -394,30 +395,27 @@ def tile_encoder_flows_pb_v_kernel(tc, flows, x_gcn1, W2, b2, dinv, grad_out, ou
                 mm(15, s, g)
             dxw(15, s)
         tok_all(G - 1)
+        tok_q(G - 1)
         dt(14)
         dt_copy(14)
         dt(15, (0,))
         dx(G - 1)
-        dx_copy(G - 1)
         dt(15, (1,))
         dt_copy(15)
-        dw(0)
-        dw(1)
-        dx_tr(G - 1)
-        dx_out(G - 1)
-        dt_q(G, 0, 1)
+        dx_copy(G - 1)
         tok(G, 0)
-        dt_q(G, 1, 2)
-        tok_q(G - 1)
+        dt_q(G)
         tok(G, 1)
-        dw(2)
-        dw(3)
+        for j in range(4):
+            dw(j)
         dx(G)
         dx_copy(G)
+        dx_tr(G - 1)
+        dx_out(G - 1)
+        dw(4)
         tok_q(G)
-        for j in range(4, GROUPS - 1):
-            dw(j)
         dx_tr(G)
         dx_out(G)
-        dw(G)
+        for j in range(5, GROUPS):
+            dw(j)
         dw_out()

@@ -6,7 +6,6 @@ from concourse.masks import make_identity
 F32 = mybir.dt.float32
 BF16 = mybir.dt.bfloat16
 U32 = mybir.dt.uint32
-I32 = mybir.dt.int32
 U8 = mybir.dt.uint8
 E4 = mybir.dt.float8_e4m3fn_x4
 E5 = mybir.dt.float8_e5m2_x4
@@ -15,14 +14,15 @@ MULT = mybir.AluOpType.mult
 
 B, N, R, I = 2, 2048, 128, 512
 P = 128
-NG = N // 512
-PAIRS = B * N // 256
+CHUNKS = N // 512
 GROUPS = B * N // 512
+STEPS = 2 * GROUPS
+STEPS_PER_GRAPH = STEPS // B
+GROUPS_PER_GRAPH = GROUPS // B
 
 FLOPS = 2 * B * N * N * I + 2 * 2 * B * N * I * R
 
-HALF = ()
-SORTED = {k: 1 if k in HALF else 2 for k in range(2, PAIRS)}
+SORTED_SLOTS = {k: 0 if k < 2 else 1 if k in (6, 8) else 2 for k in range(STEPS)}
 
 
 def tile_encoder_flows_pb_v_kernel(tc, flows, x_gcn1, W2, b2, dinv, grad_out, out_0, out_1):
@@ -37,385 +37,371 @@ def tile_encoder_flows_pb_v_kernel(tc, flows, x_gcn1, W2, b2, dinv, grad_out, ou
         ident = keep.tile([P, P], F32, name="ident", align_bytes=64)
         make_identity(nc, ident[:])
         dv = keep.tile([P, GROUPS, 4], F32, name="dv", align_bytes=64)
-        wcodes = keep.tile([P, R], U32, name="wcodes", align_bytes=64)
-        wscale = keep.tile([P, R], U8, name="wscale", align_bytes=64)
+        w_codes = keep.tile([P, R], U32, name="wcodes", align_bytes=64)
+        w_scales = keep.tile([P, R], U8, name="wscale", align_bytes=64)
 
-        raw, perm, ft, fc, fs, gr, gm, gi, gc, gs = {}, {}, {}, {}, {}, {}, {}, {}, {}, {}
-        bank, acc, D, dtb, dtbank, dtc, dts, DI, tcod, tscl = {}, {}, {}, {}, {}, {}, {}, {}, {}, {}
-        misc, xt, dxbank, xi = {}, {}, {}, {}
+        tiles = {}
 
-        def load_dv():
-            nc.scalar.dma_start(out=dv[:], in_=dinv.rearrange("b (g p t) -> p (b g) t", p=P, t=4))
+        def load_dinv(first, end, engine):
+            src = dinv.rearrange("b (g p t) -> p (b g) t", p=P, t=4)
+            engine.dma_start(out=dv[:, first:end, :], in_=src[:, first:end, :])
 
-        def load_flows(k, s=None):
-            if k not in raw:
-                raw[k] = work.tile([P, 2, N], BF16, name="raw", bufs=5, align_bytes=64)
-            b, rest = divmod(k, PAIRS // B)
-            g, h = divmod(rest, 2)
-            src = flows[b, 512 * g:512 * (g + 1), :].rearrange("(p t) c -> p t c", t=4)
-            if s is None:
-                nc.sync.dma_start(out=raw[k][:], in_=src[:, 2 * h:2 * h + 2, :])
-            else:
-                nc.sync.dma_start(out=raw[k][:, s, :], in_=src[:, 2 * h + s, :])
+        def load_flows(k, slots=(0, 2)):
+            if ("raw", k) not in tiles:
+                tiles["raw", k] = work.tile([P, 2, N], BF16, name="raw", bufs=5, align_bytes=64)
+            b, rest = divmod(k, STEPS_PER_GRAPH)
+            n, half = divmod(rest, 2)
+            src = flows[b, 512 * n:512 * (n + 1), :].rearrange("(p t) c -> p t c", t=4)
+            first, end = slots
+            nc.sync.dma_start(out=tiles["raw", k][:, first:end, :], in_=src[:, 2 * half + first:2 * half + end, :])
 
-        def load_grad(b, g, parts=1):
-            gr[b, g] = work.tile([P, 4, I], BF16, name="gr", bufs=4, align_bytes=64)
-            src = grad_out[b, 512 * g:512 * (g + 1), :].rearrange("(p j) w -> p j w", j=4)
-            n = 4 // parts
-            for i in range(parts):
-                nc.sync.dma_start(out=gr[b, g][:, n * i:n * (i + 1), :], in_=src[:, n * i:n * (i + 1), :])
+        def load_grad(b, n, parts=1):
+            tiles["grad", b, n] = work.tile([P, 4, I], BF16, name="gr", bufs=4, align_bytes=64)
+            src = grad_out[b, 512 * n:512 * (n + 1), :].rearrange("(p t) i -> p t i", t=4)
+            size = 4 // parts
+            for part in range(parts):
+                rows = slice(size * part, size * (part + 1))
+                nc.sync.dma_start(out=tiles["grad", b, n][:, rows, :], in_=src[:, rows, :])
 
         def load_w():
-            misc["w"] = keep.tile([P, I], BF16, name="wraw", align_bytes=64)
-            nc.sync.dma_start(out=misc["w"][:], in_=W2)
+            tiles["w"] = keep.tile([P, I], BF16, name="wraw", align_bytes=64)
+            nc.sync.dma_start(out=tiles["w"][:], in_=W2)
 
         def load_x():
-            misc["x"] = work.tile([P, GROUPS, 4, R], BF16, name="x", tag="raw", bufs=5, align_bytes=64)
+            tiles["x"] = work.tile([P, GROUPS, 4, R], BF16, name="x", tag="raw", bufs=5, align_bytes=64)
             for b in range(B):
-                nc.sync.dma_start(out=misc["x"][:, 4 * b:4 * b + 4], in_=x_gcn1[b].rearrange("(g p t) w -> p g t w", p=P, t=4))
+                groups = slice(GROUPS_PER_GRAPH * b, GROUPS_PER_GRAPH * (b + 1))
+                nc.sync.dma_start(out=tiles["x"][:, groups], in_=x_gcn1[b].rearrange("(g p t) w -> p g t w", p=P, t=4))
 
-        def gz_mul(b, g, js=(0, 1, 2, 3)):
-            if (b, g) not in gm:
-                gm[b, g] = work.tile([P, 4, I], BF16, name="gm", bufs=3, align_bytes=64)
-            for j in js:
-                nc.vector.tensor_scalar(out=gm[b, g][:, j, :], in0=gr[b, g][:, j, :],
-                                        scalar1=dv[:, 4 * b + g, j:j + 1], scalar2=None, op0=MULT)
-
-        def gz_int_all(b, g):
-            gi[b, g] = work.tile([P, 4 * I], BF16, name="gi", bufs=2, align_bytes=64)
-            nc.vector.tensor_copy(out=gi[b, g][:].rearrange("p (u m e j) -> p u m j e", u=2, e=2, j=4),
-                                  in_=gm[b, g][:].rearrange("p j (m u e) -> p u m j e", u=2, e=2))
-
-        def gz_int(b, g, u, eng="v"):
-            if (b, g) not in gi:
-                gi[b, g] = work.tile([P, 4 * I], BF16, name="gi", bufs=2, align_bytes=64)
-            out = gi[b, g][:, 1024 * u:1024 * (u + 1)].rearrange("p (m e j) -> p m j e", e=2, j=4)
-            src = gm[b, g][:].rearrange("p j (m u e) -> p u m j e", u=2, e=2)[:, u]
-            if eng == "v":
-                nc.vector.tensor_copy(out=out, in_=src)
-            else:
-                nc.scalar.copy(out=out, in_=src)
-
-        def gz_q(b, g):
-            gc[b, g] = keep.tile([P, I], U32, name="gc%d%d" % (b, g), align_bytes=64)
-            gs[b, g] = keep.tile([P, I], U8, name="gs%d%d" % (b, g), align_bytes=64)
-            nc.vector.quantize_mx(out=gc[b, g][:].bitcast(E5), scales=gs[b, g][:], in_=gi[b, g][:])
-
-        def sort_words(k):
-            n = SORTED.get(k, 0)
-            perm[k] = work.tile([P, 2 * NG, 2, P], F32, name="perm", bufs=2, align_bytes=64)
-            words = raw[k][:, 0:n, :].rearrange("p v c -> p (v c)").bitcast(F32)
-            nc.vector.tensor_copy(out=perm[k][:, 0:NG * n], in_=words.rearrange("p (g m u) -> p g u m", m=P, u=2))
-
-        def tr(k, s, h):
-            ps = tpool.tile([P, 4, P], F32, name="ps")
-            bank[k, s, h] = ps
-            words = raw[k][:, s, :].bitcast(F32)
-            for q in range(4):
-                g, u = 2 * h + q // 2, q % 2
-                if s < SORTED.get(k, 0):
-                    src = perm[k][:, NG * s + g, u, :]
-                else:
-                    src = words[:, 256 * g + u:256 * (g + 1):2]
-                nc.tensor.transpose(ps[:, q, :], src, ident[:])
-
-        def tr_copy(k, s, h, eng="s"):
-            if k not in ft:
-                ft[k] = work.tile([P, 8 * NG * P], BF16, name="ft", bufs=3, align_bytes=64)
-            w0 = 1024 * s + 512 * h
-            out = ft[k][:].bitcast(F32)[:, w0:w0 + 512].rearrange("p (g r u) -> p g r u", g=2, u=2)
-            src = bank[k, s, h][:].rearrange("p (g u) r -> p g r u", u=2)
-            if eng == "s":
-                nc.scalar.copy(out=out, in_=src)
-            else:
-                nc.vector.tensor_copy(out=out, in_=src)
-
-        def quant(k, a=0, z=2):
-            if k not in fc:
-                fc[k] = work.tile([P, 2 * NG * P], U32, name="fc", bufs=3, align_bytes=64)
-                fs[k] = work.tile([P, 2 * NG * P], U8, name="fs", bufs=3, align_bytes=64)
-            nc.vector.quantize_mx(out=fc[k][:, 512 * a:512 * z].bitcast(E4), scales=fs[k][:, 512 * a:512 * z], in_=ft[k][:, 2048 * a:2048 * z])
-
-        def mm(k, s, g):
-            b = k // (PAIRS // B)
-            if g == 0:
-                acc[k, s] = apool.tile([P, I], F32, name="acc")
-            cols = slice(512 * s + P * g, 512 * s + P * (g + 1))
-            nc.tensor.matmul_mx(out=acc[k, s][:], lhsT=fc[k][:, cols].bitcast(E4), lhsT_scale=fs[k][:, cols],
-                                rhs=gc[b, g][:].bitcast(E5), rhs_scale=gs[b, g][:], start=(g == 0), stop=(g == NG - 1))
-
-        def dxw(k, s, eng="s", half=None):
-            G, t = divmod(2 * k + s, 4)
-            if G not in D:
-                D[G] = work.tile([P, 4, I], BF16, name="D", bufs=4, align_bytes=64)
-            cols = slice(0, I) if half is None else slice(256 * half, 256 * (half + 1))
-            if eng == "s":
-                nc.scalar.activation(out=D[G][:, t, cols], in_=acc[k, s][:, cols], func=COPY, scale=dv[:, G, t:t + 1])
-            else:
-                nc.vector.tensor_scalar(out=D[G][:, t, cols], in0=acc[k, s][:, cols], scalar1=dv[:, G, t:t + 1],
-                                        scalar2=None, op0=MULT)
-
-        def dt(k, slots=(0, 1)):
-            if k not in dtbank:
-                ps = tpool.tile([P, 4, P], F32, name="ps")
-                dtbank[k] = ps
-            ps = dtbank[k]
-            for s in slots:
-                G, t = divmod(2 * k + s, 4)
-                words = D[G][:, t, :].bitcast(F32)
-                for u in range(2):
-                    nc.tensor.transpose(ps[:, 2 * s + u, :], words[:, P * u:P * (u + 1)], ident[:])
-
-        def dt_copy(k, slots=slice(0, 2), eng="s"):
-            G, h = divmod(k, 2)
-            if G not in dtb:
-                dtb[G] = work.tile([P, 2048], BF16, name="dtb", bufs=2, align_bytes=64)
-            out = dtb[G][:].bitcast(F32)[:, 512 * h:512 * (h + 1)].rearrange("p (v r u) -> p v r u", v=2, u=2)[:, slots]
-            src = dtbank[k][:].rearrange("p (v u) r -> p v r u", u=2)[:, slots]
-            if eng == "s":
-                nc.scalar.copy(out=out, in_=src)
-            else:
-                nc.vector.tensor_copy(out=out, in_=src)
-
-        def dt_q(G, a=0, z=2):
-            if G not in dtc:
-                dtc[G] = work.tile([P, 512], U32, name="dtc", bufs=2, align_bytes=64)
-                dts[G] = work.tile([P, 512], U8, name="dts", bufs=2, align_bytes=64)
-            cols = slice(256 * a, 256 * z)
-            nc.vector.quantize_mx(out=dtc[G][:, cols].bitcast(E5), scales=dts[G][:, cols], in_=dtb[G][:, 1024 * a:1024 * z])
-
-        def dx(G):
-            acc["dx", G] = apool.tile([P, I], F32, name="acc")
-            nc.tensor.matmul_mx(out=acc["dx", G][:], lhsT=wcodes[:].bitcast(E4), lhsT_scale=wscale[:],
-                                rhs=dtc[G][:].bitcast(E5), rhs_scale=dts[G][:], start=True, stop=True)
-
-        def dx_copy(G):
-            xt[G] = work.tile([P, I], F32, name="xt", bufs=2, align_bytes=64)
-            nc.scalar.copy(out=xt[G][:], in_=acc["dx", G][:])
-
-        def dx_tr(G):
-            ps = tpool.tile([P, 4, P], F32, name="ps")
-            dxbank[G] = ps
+        def gz_multiply(b, n):
+            tiles["gz", b, n] = work.tile([P, 4, I], BF16, name="gm", bufs=3, align_bytes=64)
             for t in range(4):
-                nc.tensor.transpose(ps[:, t, :], xt[G][:, P * t:P * (t + 1)], ident[:])
+                nc.vector.tensor_scalar(out=tiles["gz", b, n][:, t, :], in0=tiles["grad", b, n][:, t, :],
+                                        scalar1=dv[:, CHUNKS * b + n, t:t + 1], scalar2=None, op0=MULT)
 
-        def dx_out(G, eng="s"):
-            ob = work.tile([P, 4, R], F32, name="ob", bufs=2, align_bytes=64)
-            if eng == "s":
-                nc.scalar.copy(out=ob[:], in_=dxbank[G][:])
+        def gz_interleave(b, n):
+            tiles["gz4", b, n] = work.tile([P, 4 * I], BF16, name="gi", bufs=2, align_bytes=64)
+            nc.vector.tensor_copy(out=tiles["gz4", b, n][:].rearrange("p (u m e t) -> p u m t e", u=2, e=2, t=4),
+                                  in_=tiles["gz", b, n][:].rearrange("p t (m u e) -> p u m t e", u=2, e=2))
+
+        def gz_interleave_half(b, n, u, copy):
+            if u == 0:
+                tiles["gz4", b, n] = work.tile([P, 4 * I], BF16, name="gi", bufs=2, align_bytes=64)
+            out = tiles["gz4", b, n][:, 1024 * u:1024 * (u + 1)]
+            copy(out=out.rearrange("p (m e t) -> p m t e", e=2, t=4),
+                 in_=tiles["gz", b, n][:].rearrange("p t (m u e) -> p u m t e", u=2, e=2)[:, u])
+
+        def gz_quantize(b, n):
+            codes = keep.tile([P, I], U32, name="gc%d%d" % (b, n), align_bytes=64)
+            scales = keep.tile([P, I], U8, name="gs%d%d" % (b, n), align_bytes=64)
+            nc.vector.quantize_mx(out=codes[:].bitcast(E5), scales=scales[:], in_=tiles["gz4", b, n][:])
+            tiles["gz codes", b, n], tiles["gz scales", b, n] = codes, scales
+
+        def flows_sort(k):
+            slots = SORTED_SLOTS[k]
+            tiles["sorted", k] = work.tile([P, 2 * CHUNKS, 2, P], F32, name="perm", bufs=2, align_bytes=64)
+            words = tiles["raw", k][:, 0:slots, :].rearrange("p v c -> p (v c)").bitcast(F32)
+            nc.vector.tensor_copy(out=tiles["sorted", k][:, 0:CHUNKS * slots],
+                                  in_=words.rearrange("p (g m u) -> p g u m", m=P, u=2))
+
+        def flows_transpose(k, s):
+            if s == 0:
+                tiles["flows4", k] = work.tile([P, 2 * CHUNKS * P * 4], BF16, name="ft", bufs=3, align_bytes=64)
+            words = tiles["raw", k][:, s, :].bitcast(F32)
+            for half in range(2):
+                bank = tpool.tile([P, 4, P], F32, name="ps")
+                for j in range(4):
+                    n, u = 2 * half + j // 2, j % 2
+                    if s < SORTED_SLOTS[k]:
+                        src = tiles["sorted", k][:, CHUNKS * s + n, u, :]
+                    else:
+                        src = words[:, 256 * n + u:256 * (n + 1):2]
+                    nc.tensor.transpose(bank[:, j, :], src, ident[:])
+                first = 1024 * s + 512 * half
+                out = tiles["flows4", k][:].bitcast(F32)[:, first:first + 512]
+                nc.scalar.copy(out=out.rearrange("p (g r u) -> p g r u", g=2, u=2),
+                               in_=bank[:].rearrange("p (g u) r -> p g r u", u=2))
+
+        def flows_quantize(k, slots=(0, 2)):
+            first, end = slots
+            if first == 0:
+                tiles["flows codes", k] = work.tile([P, 2 * CHUNKS * P], U32, name="fc", bufs=3, align_bytes=64)
+                tiles["flows scales", k] = work.tile([P, 2 * CHUNKS * P], U8, name="fs", bufs=3, align_bytes=64)
+            words = slice(512 * first, 512 * end)
+            nc.vector.quantize_mx(out=tiles["flows codes", k][:, words].bitcast(E4),
+                                  scales=tiles["flows scales", k][:, words],
+                                  in_=tiles["flows4", k][:, 2048 * first:2048 * end])
+
+        def aggregate(k, s, chunks=range(CHUNKS)):
+            b = k // STEPS_PER_GRAPH
+            for n in chunks:
+                if n == 0:
+                    tiles["dmsg", k, s] = apool.tile([P, I], F32, name="acc")
+                cols = slice(512 * s + P * n, 512 * s + P * (n + 1))
+                nc.tensor.matmul_mx(out=tiles["dmsg", k, s][:],
+                                    lhsT=tiles["flows codes", k][:, cols].bitcast(E4),
+                                    lhsT_scale=tiles["flows scales", k][:, cols],
+                                    rhs=tiles["gz codes", b, n][:].bitcast(E5), rhs_scale=tiles["gz scales", b, n][:],
+                                    start=(n == 0), stop=(n == CHUNKS - 1))
+
+        def dxw_rows(k, s, on_vector=False):
+            g, t = divmod(2 * k + s, 4)
+            if t == 0:
+                tiles["dxw", g] = work.tile([P, 4, I], BF16, name="D", bufs=4, align_bytes=64)
+            if on_vector:
+                nc.vector.tensor_scalar(out=tiles["dxw", g][:, t, :], in0=tiles["dmsg", k, s][:],
+                                        scalar1=dv[:, g, t:t + 1], scalar2=None, op0=MULT)
             else:
-                nc.vector.tensor_copy(out=ob[:], in_=dxbank[G][:])
-            b, g = divmod(G, GROUPS // B)
-            dst = out_0[b, 512 * g:512 * (g + 1), :].rearrange("(p t) w -> p t w", t=4)
-            nc.sync.dma_start(out=dst, in_=ob[:])
+                nc.scalar.activation(out=tiles["dxw", g][:, t, :], in_=tiles["dmsg", k, s][:], func=COPY,
+                                     scale=dv[:, g, t:t + 1])
 
-        def tok_all(G):
-            DI[G] = work.tile([P, 4 * I], BF16, name="DI", bufs=2, align_bytes=64)
-            nc.vector.tensor_copy(out=DI[G][:].rearrange("p (c i t) -> p c t i", i=4, t=4),
-                                  in_=D[G][:].rearrange("p t (c i) -> p c t i", i=4))
+        def dxw_transpose(k, slots=(0, 1)):
+            if 0 in slots:
+                tiles["dxwT bank", k] = tpool.tile([P, 4, P], F32, name="ps")
+            for s in slots:
+                g, t = divmod(2 * k + s, 4)
+                words = tiles["dxw", g][:, t, :].bitcast(F32)
+                for u in range(2):
+                    nc.tensor.transpose(tiles["dxwT bank", k][:, 2 * s + u, :], words[:, P * u:P * (u + 1)], ident[:])
 
-        def tok(G, h, eng="v"):
-            if G not in DI:
-                DI[G] = work.tile([P, 4 * I], BF16, name="DI", bufs=2, align_bytes=64)
-            out = DI[G][:, 1024 * h:1024 * (h + 1)].rearrange("p (c i t) -> p c t i", i=4, t=4)
-            src = D[G][:, :, 256 * h:256 * (h + 1)].rearrange("p t (c i) -> p c t i", i=4)
-            if eng == "v":
-                nc.vector.tensor_copy(out=out, in_=src)
-            else:
-                nc.scalar.copy(out=out, in_=src)
+        def dxw_transpose_copy(k):
+            g, half = divmod(k, 2)
+            if half == 0:
+                tiles["dxwT4", g] = work.tile([P, 4 * I], BF16, name="dtb", bufs=2, align_bytes=64)
+            out = tiles["dxwT4", g][:].bitcast(F32)[:, 512 * half:512 * (half + 1)]
+            nc.scalar.copy(out=out.rearrange("p (v r u) -> p v r u", v=2, u=2),
+                           in_=tiles["dxwT bank", k][:].rearrange("p (v u) r -> p v r u", u=2))
 
-        def tok_q(G):
-            tcod[G] = keep.tile([P, I], U32, name="tc%d" % G, align_bytes=64)
-            tscl[G] = keep.tile([P, I], U8, name="ts%d" % G, align_bytes=64)
-            nc.vector.quantize_mx(out=tcod[G][:].bitcast(E5), scales=tscl[G][:], in_=DI[G][:])
+        def dxw_transpose_quantize(g):
+            codes = work.tile([P, I], U32, name="dtc", bufs=2, align_bytes=64)
+            scales = work.tile([P, I], U8, name="dts", bufs=2, align_bytes=64)
+            nc.vector.quantize_mx(out=codes[:].bitcast(E5), scales=scales[:], in_=tiles["dxwT4", g][:])
+            tiles["dxwT codes", g], tiles["dxwT scales", g] = codes, scales
 
-        def x_int(i):
-            b = i // 2
-            if b not in xi:
-                xi[b] = work.tile([P, 4, R, 4], BF16, name="xi", tag="gi", bufs=2, align_bytes=64)
-            for g in range(2):
-                src = misc["x"][:, 2 * i + g].rearrange("p t (c i) -> p c t i", i=4)
-                nc.vector.tensor_copy(out=xi[b][:, 2 * (i % 2) + g].rearrange("p (c i) t -> p c t i", i=4), in_=src)
+        def dx_product(g):
+            bank = apool.tile([P, I], F32, name="acc")
+            nc.tensor.matmul_mx(out=bank[:], lhsT=w_codes[:].bitcast(E4), lhsT_scale=w_scales[:],
+                                rhs=tiles["dxwT codes", g][:].bitcast(E5), rhs_scale=tiles["dxwT scales", g][:],
+                                start=True, stop=True)
+            tiles["dxT bank", g] = bank
 
-        def x_q(b):
-            if b == 0:
-                misc["xc"] = keep.tile([P, GROUPS * R], U32, name="xc", align_bytes=64)
-                misc["xs"] = keep.tile([P, GROUPS * R], U8, name="xs", align_bytes=64)
-            cols = slice(512 * b, 512 * (b + 1))
-            nc.vector.quantize_mx(out=misc["xc"][:, cols].bitcast(E4), scales=misc["xs"][:, cols], in_=xi[b][:].rearrange("p g w t -> p (g w t)"))
+        def dx_copy(g):
+            tiles["dxT", g] = work.tile([P, I], F32, name="xt", bufs=2, align_bytes=64)
+            nc.scalar.copy(out=tiles["dxT", g][:], in_=tiles["dxT bank", g][:])
 
-        def dw(G):
-            if G == 0:
-                acc["dw"] = apool.tile([P, I], F32, name="acc")
-            cols = slice(R * G, R * (G + 1))
-            nc.tensor.matmul_mx(out=acc["dw"][:], lhsT=misc["xc"][:, cols].bitcast(E4), lhsT_scale=misc["xs"][:, cols],
-                                rhs=tcod[G][:].bitcast(E5), rhs_scale=tscl[G][:], start=(G == 0), stop=(G == GROUPS - 1))
+        def dx_transpose(g):
+            tiles["dx bank", g] = tpool.tile([P, 4, P], F32, name="ps")
+            for t in range(4):
+                nc.tensor.transpose(tiles["dx bank", g][:, t, :], tiles["dxT", g][:, P * t:P * (t + 1)], ident[:])
 
-        def dw_out():
-            wo = work.tile([P, I], F32, name="wo", bufs=1, align_bytes=64)
-            nc.vector.tensor_copy(out=wo[:].rearrange("p (m u e) -> p m u e", u=2, e=2),
-                                  in_=acc["dw"][:].rearrange("p (u m e) -> p m u e", u=2, e=2))
-            nc.sync.dma_start(out=out_1, in_=wo[:])
+        def dx_store(g):
+            rows = work.tile([P, 4, R], F32, name="ob", bufs=2, align_bytes=64)
+            nc.scalar.copy(out=rows[:], in_=tiles["dx bank", g][:])
+            b, n = divmod(g, GROUPS_PER_GRAPH)
+            nc.sync.dma_start(out=out_0[b, 512 * n:512 * (n + 1), :].rearrange("(p t) w -> p t w", t=4), in_=rows[:])
 
-        def w_tr():
-            ps = tpool.tile([P, 4, P], F32, name="ps")
-            misc["wps"] = ps
-            words = misc["w"][:].bitcast(F32)
+        def w_transpose():
+            bank = tpool.tile([P, 4, P], F32, name="ps")
+            words = tiles["w"][:].bitcast(F32)
             for u in range(2):
-                nc.tensor.transpose(ps[:, u, :], words[:, u:256:2], ident[:])
+                nc.tensor.transpose(bank[:, u, :], words[:, u:256:2], ident[:])
+            tiles["w4"] = keep.tile([P, 4 * R], BF16, name="wi", align_bytes=64)
+            nc.scalar.copy(out=tiles["w4"][:].bitcast(F32).rearrange("p (r u) -> p r u", u=2),
+                           in_=bank[:, 0:2, :].rearrange("p u r -> p r u"))
 
-        def w_copy():
-            misc["wi"] = keep.tile([P, 4 * R], BF16, name="wi", align_bytes=64)
-            nc.scalar.copy(out=misc["wi"][:].bitcast(F32).rearrange("p (r u) -> p r u", u=2),
-                           in_=misc["wps"][:, 0:2, :].rearrange("p u r -> p r u"))
+        def w_quantize():
+            nc.vector.quantize_mx(out=w_codes[:].bitcast(E4), scales=w_scales[:], in_=tiles["w4"][:])
 
-        def w_q():
-            nc.vector.quantize_mx(out=wcodes[:].bitcast(E4), scales=wscale[:], in_=misc["wi"][:])
+        def dxw_interleave(g):
+            tiles["dxw4", g] = work.tile([P, 4 * I], BF16, name="DI", bufs=2, align_bytes=64)
+            nc.vector.tensor_copy(out=tiles["dxw4", g][:].rearrange("p (c i t) -> p c t i", i=4, t=4),
+                                  in_=tiles["dxw", g][:].rearrange("p t (c i) -> p c t i", i=4))
 
-        load_dv()
-        load_grad(0, 0, 2)
-        load_flows(0, 0)
+        def dxw_interleave_half(g, half):
+            if half == 0:
+                tiles["dxw4", g] = work.tile([P, 4 * I], BF16, name="DI", bufs=2, align_bytes=64)
+            out = tiles["dxw4", g][:, 1024 * half:1024 * (half + 1)]
+            src = tiles["dxw", g][:, :, 256 * half:256 * (half + 1)]
+            nc.vector.tensor_copy(out=out.rearrange("p (c i t) -> p c t i", i=4, t=4),
+                                  in_=src.rearrange("p t (c i) -> p c t i", i=4))
+
+        def dxw_quantize(g):
+            codes = keep.tile([P, I], U32, name="tc%d" % g, align_bytes=64)
+            scales = keep.tile([P, I], U8, name="ts%d" % g, align_bytes=64)
+            nc.vector.quantize_mx(out=codes[:].bitcast(E5), scales=scales[:], in_=tiles["dxw4", g][:])
+            tiles["dxw codes", g], tiles["dxw scales", g] = codes, scales
+
+        def x_interleave(two):
+            b, pair = divmod(two, 2)
+            if pair == 0:
+                tiles["x4", b] = work.tile([P, GROUPS_PER_GRAPH, R, 4], BF16, name="xi", tag="gi", bufs=2,
+                                           align_bytes=64)
+            for j in range(2):
+                src = tiles["x"][:, 2 * two + j].rearrange("p t (c i) -> p c t i", i=4)
+                out = tiles["x4", b][:, 2 * pair + j].rearrange("p (c i) t -> p c t i", i=4)
+                nc.vector.tensor_copy(out=out, in_=src)
+
+        def x_quantize(b):
+            if b == 0:
+                tiles["x codes"] = keep.tile([P, GROUPS * R], U32, name="xc", align_bytes=64)
+                tiles["x scales"] = keep.tile([P, GROUPS * R], U8, name="xs", align_bytes=64)
+            words = slice(GROUPS_PER_GRAPH * R * b, GROUPS_PER_GRAPH * R * (b + 1))
+            nc.vector.quantize_mx(out=tiles["x codes"][:, words].bitcast(E4), scales=tiles["x scales"][:, words],
+                                  in_=tiles["x4", b][:].rearrange("p g w t -> p (g w t)"))
+
+        def dw_product(g):
+            if g == 0:
+                tiles["dw"] = apool.tile([P, I], F32, name="acc")
+            cols = slice(R * g, R * (g + 1))
+            nc.tensor.matmul_mx(out=tiles["dw"][:], lhsT=tiles["x codes"][:, cols].bitcast(E4),
+                                lhsT_scale=tiles["x scales"][:, cols],
+                                rhs=tiles["dxw codes", g][:].bitcast(E5), rhs_scale=tiles["dxw scales", g][:],
+                                start=(g == 0), stop=(g == GROUPS - 1))
+
+        def dw_store():
+            rows = work.tile([P, I], F32, name="wo", bufs=1, align_bytes=64)
+            nc.vector.tensor_copy(out=rows[:].rearrange("p (m u e) -> p m u e", u=2, e=2),
+                                  in_=tiles["dw"][:].rearrange("p (u m e) -> p m u e", u=2, e=2))
+            nc.sync.dma_start(out=out_1, in_=rows[:])
+
+        load_dinv(0, 2, nc.scalar)
+        load_grad(0, 0, parts=2)
+        load_flows(0, (0, 1))
         load_grad(0, 1)
-        load_flows(0, 1)
+        load_dinv(2, 4, nc.sync)
+        load_flows(0, (1, 2))
         load_grad(0, 2)
-        load_flows(1, 0)
+        load_flows(1, (0, 1))
         load_grad(0, 3)
-        load_flows(1, 1)
+        load_flows(1, (1, 2))
+        load_dinv(4, 8, nc.sync)
         load_flows(2)
         load_w()
+
+        gz_multiply(0, 0)
+        gz_interleave_half(0, 0, 0, nc.vector.tensor_copy)
+        gz_interleave_half(0, 0, 1, nc.scalar.copy)
+        flows_transpose(0, 0)
+        gz_multiply(0, 1)
+        gz_quantize(0, 0)
+        gz_interleave_half(0, 1, 0, nc.vector.tensor_copy)
+        gz_interleave_half(0, 1, 1, nc.scalar.copy)
+        flows_quantize(0, (0, 1))
+        flows_transpose(0, 1)
+        gz_multiply(0, 2)
+        gz_quantize(0, 1)
+        aggregate(0, 0, (0, 1))
+        gz_interleave_half(0, 2, 0, nc.vector.tensor_copy)
+        gz_interleave_half(0, 2, 1, nc.scalar.copy)
+        flows_quantize(0, (1, 2))
+        gz_multiply(0, 3)
         load_flows(3)
+        load_grad(1, 0)
         load_flows(4)
-
-        def trs(k, s):
-            for h in range(2):
-                tr(k, s, h)
-                tr_copy(k, s, h)
-
-        def mms(slots, gs_):
-            for g in gs_:
-                for k, s in slots:
-                    mm(k, s, g)
-
-        gz_mul(0, 0)
-        gz_int(0, 0, 0)
-        gz_int(0, 0, 1, "s")
-        trs(0, 0)
-        gz_mul(0, 1)
-        gz_q(0, 0)
-        gz_int(0, 1, 0)
-        gz_int(0, 1, 1, "s")
-        quant(0, 0, 1)
-        trs(0, 1)
-        gz_mul(0, 2)
-        gz_q(0, 1)
-        mms([(0, 0)], (0, 1))
-        gz_int(0, 2, 0)
-        gz_int(0, 2, 1, "s")
-        quant(0, 1, 2)
-        gz_mul(0, 3)
-        gz_q(0, 2)
-        trs(1, 0)
-        mms([(0, 1)], (0, 1))
-        gz_int(0, 3, 0)
-        gz_int(0, 3, 1, "s")
-        trs(1, 1)
-        mms([(0, 0), (0, 1)], (2,))
-        quant(1, 0, 1)
-        gz_q(0, 3)
-        sort_words(2)
-        mms([(0, 0), (0, 1)], (3,))
-        quant(1, 1, 2)
-        mms([(1, 0)], range(4))
-        trs(2, 0)
-        dxw(0, 0, "v")
-        dxw(0, 1, "v")
-        trs(2, 1)
-        dxw(1, 0)
-        sort_words(3)
-        mms([(1, 1)], range(4))
-        w_tr()
-        w_copy()
-        quant(2)
-        dxw(1, 1)
-
+        load_grad(1, 1)
+        gz_quantize(0, 2)
+        flows_transpose(1, 0)
+        aggregate(0, 1, (0, 1))
+        gz_interleave_half(0, 3, 0, nc.vector.tensor_copy)
+        gz_interleave_half(0, 3, 1, nc.scalar.copy)
+        flows_transpose(1, 1)
+        aggregate(0, 0, (2,))
+        aggregate(0, 1, (2,))
+        flows_quantize(1, (0, 1))
+        gz_quantize(0, 3)
+        flows_sort(2)
+        aggregate(0, 0, (3,))
+        aggregate(0, 1, (3,))
+        flows_quantize(1, (1, 2))
+        aggregate(1, 0)
+        flows_transpose(2, 0)
+        dxw_rows(0, 0, on_vector=True)
+        dxw_rows(0, 1, on_vector=True)
+        flows_transpose(2, 1)
+        dxw_rows(1, 0)
+        flows_sort(3)
+        gz_multiply(1, 0)
+        aggregate(1, 1)
+        w_transpose()
+        flows_quantize(2)
+        dxw_rows(1, 1)
         load_flows(5)
-        plan = {
-            3: ["sort", "quant", (gz_mul, 1, 0), (dt_q, 0), (gz_int_all, 1, 0)],
-            4: ["sort", (gz_mul, 1, 1), (gz_q, 1, 0), "quant", (tok_all, 0)],
-            5: ["sort", (gz_int_all, 1, 1), "quant", (dt_q, 1), (tok_q, 0)],
-            6: ["sort", (gz_mul, 1, 2), (gz_q, 1, 1), "quant", (gz_int_all, 1, 2), (gz_mul, 1, 3)],
-            7: ["sort", (gz_q, 1, 2), "quant", (dt_q, 2), (gz_int_all, 1, 3)],
-            8: ["sort", (gz_q, 1, 3), "quant", (tok_all, 1)],
-            9: ["sort", (tok_q, 1), "quant", (dt_q, 3), (tok_all, 2)],
-            10: ["sort", (tok_q, 2), "quant", (tok_all, 3)],
-            11: ["sort", (tok_q, 3), "quant", (dt_q, 4)],
-            12: [(tok_all, 4), "sort", "quant", (tok_q, 4)],
-            13: ["sort", (x_int, 0), "quant", (dt_q, 5), (x_int, 1)],
-            14: [(tok_all, 5), "sort", (x_q, 0), "quant", (tok_q, 5)],
-            15: [(x_int, 2), (x_int, 3), "quant", (x_q, 1), (dt_q, 6)],
+
+        vector_work = {
+            3: [(flows_sort, 4), (gz_interleave, 1, 0), (flows_quantize, 3), (gz_multiply, 1, 1),
+                (dxw_transpose_quantize, 0), (gz_quantize, 1, 0)],
+            4: [(flows_sort, 5), (gz_interleave, 1, 1), (flows_quantize, 4), (dxw_interleave, 0)],
+            5: [(flows_sort, 6), (gz_multiply, 1, 2), (gz_quantize, 1, 1), (flows_quantize, 5),
+                (dxw_transpose_quantize, 1), (dxw_quantize, 0)],
+            6: [(flows_sort, 7), (gz_interleave, 1, 2), (flows_quantize, 6), (gz_multiply, 1, 3), (gz_quantize, 1, 2)],
+            7: [(flows_sort, 8), (gz_interleave, 1, 3), (flows_quantize, 7), (dxw_transpose_quantize, 2)],
+            8: [(flows_sort, 9), (gz_quantize, 1, 3), (flows_quantize, 8), (dxw_interleave, 1)],
+            9: [(flows_sort, 10), (dxw_quantize, 1), (flows_quantize, 9), (dxw_transpose_quantize, 3),
+                (dxw_interleave, 2)],
+            10: [(flows_sort, 11), (dxw_quantize, 2), (flows_quantize, 10), (dxw_interleave, 3)],
+            11: [(flows_sort, 12), (dxw_quantize, 3), (flows_quantize, 11), (dxw_transpose_quantize, 4)],
+            12: [(dxw_interleave, 4), (flows_sort, 13), (flows_quantize, 12), (dxw_quantize, 4)],
+            13: [(flows_sort, 14), (x_interleave, 0), (flows_quantize, 13), (dxw_transpose_quantize, 5),
+                 (x_interleave, 1)],
+            14: [(dxw_interleave, 5), (flows_sort, 15), (x_quantize, 0), (flows_quantize, 14), (dxw_quantize, 5)],
+            15: [(x_interleave, 2), (x_interleave, 3), (flows_quantize, 15), (x_quantize, 1),
+                 (dxw_transpose_quantize, 6)],
         }
-        for k in range(3, PAIRS):
-            G, odd = divmod(k - 3, 2)
-            if k + 3 < PAIRS:
+        for k in range(3, STEPS):
+            if k + 3 < STEPS:
                 load_flows(k + 3)
-            elif k + 3 == PAIRS:
+            elif k + 3 == STEPS:
                 load_x()
             if k == 3:
-                for g in range(NG):
-                    load_grad(1, g)
-            trs(k, 0)
-            trs(k, 1)
-            dts_now = [0, 1] if k == 3 else [k - 2]
-            for j in dts_now:
-                dt(j)
-                dt_copy(j)
-            if odd == 0 and G > 0:
-                dx_tr(G - 1)
-                dx_out(G - 1)
-            if odd == 1:
-                dx(G)
-                dx_copy(G)
+                load_grad(1, 2)
+                load_grad(1, 3)
+
+            flows_transpose(k, 0)
+            flows_transpose(k, 1)
+            for j in (0, 1) if k == 3 else (k - 2,):
+                dxw_transpose(j)
+                dxw_transpose_copy(j)
+            if k % 2 == 1 and k > 3:
+                dx_transpose((k - 5) // 2)
+                dx_store((k - 5) // 2)
+            if k % 2 == 0:
+                dx_product((k - 4) // 2)
+                dx_copy((k - 4) // 2)
             for s in range(2):
-                for g in range(NG):
-                    mm(k - 1, s, g)
-                dxw(k - 1, s)
+                aggregate(k - 1, s)
+                dxw_rows(k - 1, s)
+
             if k == 3:
-                w_q()
-            for item in plan[k]:
-                if item == "sort":
-                    if k + 1 < PAIRS:
-                        sort_words(k + 1)
-                elif item == "quant":
-                    quant(k)
-                else:
-                    item[0](*item[1:])
-        G = GROUPS - 1
+                w_quantize()
+            for call, *arguments in vector_work[k]:
+                call(*arguments)
+
+        last = GROUPS - 1
         for s in range(2):
-            for g in range(NG):
-                mm(15, s, g)
-            dxw(15, s)
-        tok_all(G - 1)
-        tok_q(G - 1)
-        dt(14)
-        dt_copy(14)
-        dt(15, (0,))
-        dx(G - 1)
-        dt(15, (1,))
-        dt_copy(15)
-        dx_copy(G - 1)
-        tok(G, 0)
-        dt_q(G)
-        tok(G, 1)
-        for j in range(4):
-            dw(j)
-        dx(G)
-        dx_copy(G)
-        dx_tr(G - 1)
-        dx_out(G - 1)
-        dw(4)
-        tok_q(G)
-        dx_tr(G)
-        dx_out(G)
-        for j in range(5, GROUPS):
-            dw(j)
-        dw_out()
+            aggregate(STEPS - 1, s)
+            dxw_rows(STEPS - 1, s)
+        dxw_interleave(last - 1)
+        dxw_quantize(last - 1)
+        dxw_transpose(STEPS - 2)
+        dxw_transpose_copy(STEPS - 2)
+        dxw_transpose(STEPS - 1, (0,))
+        dx_product(last - 1)
+        dxw_transpose(STEPS - 1, (1,))
+        dxw_transpose_copy(STEPS - 1)
+        dx_copy(last - 1)
+        dxw_interleave_half(last, 0)
+        dxw_transpose_quantize(last)
+        dxw_interleave_half(last, 1)
+        for g in range(4):
+            dw_product(g)
+        dx_product(last)
+        dx_copy(last)
+        dx_transpose(last - 1)
+        dx_store(last - 1)
+        dw_product(4)
+        dxw_quantize(last)
+        dx_transpose(last)
+        dx_store(last)
+        for g in range(5, GROUPS):
+            dw_product(g)
+        dw_store()

from contextlib import ExitStack

import concourse.mybir as mybir
from concourse.masks import make_identity

F32 = mybir.dt.float32
BF16 = mybir.dt.bfloat16
U32 = mybir.dt.uint32
U8 = mybir.dt.uint8
E4 = mybir.dt.float8_e4m3fn_x4
E5 = mybir.dt.float8_e5m2_x4
COPY = mybir.ActivationFunctionType.Copy
MULT = mybir.AluOpType.mult

B, N, R, I = 2, 2048, 128, 512
P = 128
CHUNKS = N // 512
GROUPS = B * N // 512
STEPS = 2 * GROUPS
STEPS_PER_GRAPH = STEPS // B
GROUPS_PER_GRAPH = GROUPS // B

FLOPS = 2 * B * N * N * I + 2 * 2 * B * N * I * R

SORTED_SLOTS = {k: 0 if k < 2 else 1 if k in (6, 8) else 2 for k in range(STEPS)}


def tile_encoder_flows_pb_v_kernel(tc, flows, x_gcn1, W2, b2, dinv, grad_out, out_0, out_1):
    nc = tc.nc
    with ExitStack() as ctx:
        keep = ctx.enter_context(tc.tile_pool(name="keep", bufs=1))
        work = ctx.enter_context(tc.tile_pool(name="work", bufs=2))
        tpool = ctx.enter_context(tc.psum_pool(name="tpool", bufs=5))
        apool = ctx.enter_context(tc.psum_pool(name="apool", bufs=3))
        ctx.enter_context(tc.manual_schedule())

        ident = keep.tile([P, P], F32, name="ident", align_bytes=64)
        make_identity(nc, ident[:])
        dv = keep.tile([P, GROUPS, 4], F32, name="dv", align_bytes=64)
        w_codes = keep.tile([P, R], U32, name="wcodes", align_bytes=64)
        w_scales = keep.tile([P, R], U8, name="wscale", align_bytes=64)

        tiles = {}

        def load_dinv(first, end, engine):
            src = dinv.rearrange("b (g p t) -> p (b g) t", p=P, t=4)
            engine.dma_start(out=dv[:, first:end, :], in_=src[:, first:end, :])

        def load_flows(k, slots=(0, 2)):
            if ("raw", k) not in tiles:
                tiles["raw", k] = work.tile([P, 2, N], BF16, name="raw", bufs=5, align_bytes=64)
            b, rest = divmod(k, STEPS_PER_GRAPH)
            n, half = divmod(rest, 2)
            src = flows[b, 512 * n:512 * (n + 1), :].rearrange("(p t) c -> p t c", t=4)
            first, end = slots
            nc.sync.dma_start(out=tiles["raw", k][:, first:end, :], in_=src[:, 2 * half + first:2 * half + end, :])

        def load_grad(b, n, parts=1):
            tiles["grad", b, n] = work.tile([P, 4, I], BF16, name="gr", bufs=4, align_bytes=64)
            src = grad_out[b, 512 * n:512 * (n + 1), :].rearrange("(p t) i -> p t i", t=4)
            size = 4 // parts
            for part in range(parts):
                rows = slice(size * part, size * (part + 1))
                nc.sync.dma_start(out=tiles["grad", b, n][:, rows, :], in_=src[:, rows, :])

        def load_w():
            tiles["w"] = keep.tile([P, I], BF16, name="wraw", align_bytes=64)
            nc.sync.dma_start(out=tiles["w"][:], in_=W2)

        def load_x():
            tiles["x"] = work.tile([P, GROUPS, 4, R], BF16, name="x", tag="raw", bufs=5, align_bytes=64)
            for b in range(B):
                groups = slice(GROUPS_PER_GRAPH * b, GROUPS_PER_GRAPH * (b + 1))
                nc.sync.dma_start(out=tiles["x"][:, groups], in_=x_gcn1[b].rearrange("(g p t) w -> p g t w", p=P, t=4))

        def gz_multiply(b, n):
            tiles["gz", b, n] = work.tile([P, 4, I], BF16, name="gm", bufs=3, align_bytes=64)
            for t in range(4):
                nc.vector.tensor_scalar(out=tiles["gz", b, n][:, t, :], in0=tiles["grad", b, n][:, t, :],
                                        scalar1=dv[:, CHUNKS * b + n, t:t + 1], scalar2=None, op0=MULT)

        def gz_interleave(b, n):
            tiles["gz4", b, n] = work.tile([P, 4 * I], BF16, name="gi", bufs=2, align_bytes=64)
            nc.vector.tensor_copy(out=tiles["gz4", b, n][:].rearrange("p (u m e t) -> p u m t e", u=2, e=2, t=4),
                                  in_=tiles["gz", b, n][:].rearrange("p t (m u e) -> p u m t e", u=2, e=2))

        def gz_interleave_half(b, n, u, copy):
            if u == 0:
                tiles["gz4", b, n] = work.tile([P, 4 * I], BF16, name="gi", bufs=2, align_bytes=64)
            out = tiles["gz4", b, n][:, 1024 * u:1024 * (u + 1)]
            copy(out=out.rearrange("p (m e t) -> p m t e", e=2, t=4),
                 in_=tiles["gz", b, n][:].rearrange("p t (m u e) -> p u m t e", u=2, e=2)[:, u])

        def gz_quantize(b, n):
            codes = keep.tile([P, I], U32, name="gc%d%d" % (b, n), align_bytes=64)
            scales = keep.tile([P, I], U8, name="gs%d%d" % (b, n), align_bytes=64)
            nc.vector.quantize_mx(out=codes[:].bitcast(E5), scales=scales[:], in_=tiles["gz4", b, n][:])
            tiles["gz codes", b, n], tiles["gz scales", b, n] = codes, scales

        def flows_sort(k):
            slots = SORTED_SLOTS[k]
            tiles["sorted", k] = work.tile([P, 2 * CHUNKS, 2, P], F32, name="perm", bufs=2, align_bytes=64)
            words = tiles["raw", k][:, 0:slots, :].rearrange("p v c -> p (v c)").bitcast(F32)
            nc.vector.tensor_copy(out=tiles["sorted", k][:, 0:CHUNKS * slots],
                                  in_=words.rearrange("p (g m u) -> p g u m", m=P, u=2))

        def flows_transpose(k, s):
            if s == 0:
                tiles["flows4", k] = work.tile([P, 2 * CHUNKS * P * 4], BF16, name="ft", bufs=3, align_bytes=64)
            words = tiles["raw", k][:, s, :].bitcast(F32)
            for half in range(2):
                bank = tpool.tile([P, 4, P], F32, name="ps")
                for j in range(4):
                    n, u = 2 * half + j // 2, j % 2
                    if s < SORTED_SLOTS[k]:
                        src = tiles["sorted", k][:, CHUNKS * s + n, u, :]
                    else:
                        src = words[:, 256 * n + u:256 * (n + 1):2]
                    nc.tensor.transpose(bank[:, j, :], src, ident[:])
                first = 1024 * s + 512 * half
                out = tiles["flows4", k][:].bitcast(F32)[:, first:first + 512]
                nc.scalar.copy(out=out.rearrange("p (g r u) -> p g r u", g=2, u=2),
                               in_=bank[:].rearrange("p (g u) r -> p g r u", u=2))

        def flows_quantize(k, slots=(0, 2)):
            first, end = slots
            if first == 0:
                tiles["flows codes", k] = work.tile([P, 2 * CHUNKS * P], U32, name="fc", bufs=3, align_bytes=64)
                tiles["flows scales", k] = work.tile([P, 2 * CHUNKS * P], U8, name="fs", bufs=3, align_bytes=64)
            words = slice(512 * first, 512 * end)
            nc.vector.quantize_mx(out=tiles["flows codes", k][:, words].bitcast(E4),
                                  scales=tiles["flows scales", k][:, words],
                                  in_=tiles["flows4", k][:, 2048 * first:2048 * end])

        def aggregate(k, s, chunks=range(CHUNKS)):
            b = k // STEPS_PER_GRAPH
            for n in chunks:
                if n == 0:
                    tiles["dmsg", k, s] = apool.tile([P, I], F32, name="acc")
                cols = slice(512 * s + P * n, 512 * s + P * (n + 1))
                nc.tensor.matmul_mx(out=tiles["dmsg", k, s][:],
                                    lhsT=tiles["flows codes", k][:, cols].bitcast(E4),
                                    lhsT_scale=tiles["flows scales", k][:, cols],
                                    rhs=tiles["gz codes", b, n][:].bitcast(E5), rhs_scale=tiles["gz scales", b, n][:],
                                    start=(n == 0), stop=(n == CHUNKS - 1))

        def dxw_rows(k, s, on_vector=False):
            g, t = divmod(2 * k + s, 4)
            if t == 0:
                tiles["dxw", g] = work.tile([P, 4, I], BF16, name="D", bufs=4, align_bytes=64)
            if on_vector:
                nc.vector.tensor_scalar(out=tiles["dxw", g][:, t, :], in0=tiles["dmsg", k, s][:],
                                        scalar1=dv[:, g, t:t + 1], scalar2=None, op0=MULT)
            else:
                nc.scalar.activation(out=tiles["dxw", g][:, t, :], in_=tiles["dmsg", k, s][:], func=COPY,
                                     scale=dv[:, g, t:t + 1])

        def dxw_transpose(k, slots=(0, 1)):
            if 0 in slots:
                tiles["dxwT bank", k] = tpool.tile([P, 4, P], F32, name="ps")
            for s in slots:
                g, t = divmod(2 * k + s, 4)
                words = tiles["dxw", g][:, t, :].bitcast(F32)
                for u in range(2):
                    nc.tensor.transpose(tiles["dxwT bank", k][:, 2 * s + u, :], words[:, P * u:P * (u + 1)], ident[:])

        def dxw_transpose_copy(k):
            g, half = divmod(k, 2)
            if half == 0:
                tiles["dxwT4", g] = work.tile([P, 4 * I], BF16, name="dtb", bufs=2, align_bytes=64)
            out = tiles["dxwT4", g][:].bitcast(F32)[:, 512 * half:512 * (half + 1)]
            nc.scalar.copy(out=out.rearrange("p (v r u) -> p v r u", v=2, u=2),
                           in_=tiles["dxwT bank", k][:].rearrange("p (v u) r -> p v r u", u=2))

        def dxw_transpose_quantize(g):
            codes = work.tile([P, I], U32, name="dtc", bufs=2, align_bytes=64)
            scales = work.tile([P, I], U8, name="dts", bufs=2, align_bytes=64)
            nc.vector.quantize_mx(out=codes[:].bitcast(E5), scales=scales[:], in_=tiles["dxwT4", g][:])
            tiles["dxwT codes", g], tiles["dxwT scales", g] = codes, scales

        def dx_product(g):
            bank = apool.tile([P, I], F32, name="acc")
            nc.tensor.matmul_mx(out=bank[:], lhsT=w_codes[:].bitcast(E4), lhsT_scale=w_scales[:],
                                rhs=tiles["dxwT codes", g][:].bitcast(E5), rhs_scale=tiles["dxwT scales", g][:],
                                start=True, stop=True)
            tiles["dxT bank", g] = bank

        def dx_copy(g):
            tiles["dxT", g] = work.tile([P, I], F32, name="xt", bufs=2, align_bytes=64)
            nc.scalar.copy(out=tiles["dxT", g][:], in_=tiles["dxT bank", g][:])

        def dx_transpose(g):
            tiles["dx bank", g] = tpool.tile([P, 4, P], F32, name="ps")
            for t in range(4):
                nc.tensor.transpose(tiles["dx bank", g][:, t, :], tiles["dxT", g][:, P * t:P * (t + 1)], ident[:])

        def dx_store(g):
            rows = work.tile([P, 4, R], F32, name="ob", bufs=2, align_bytes=64)
            nc.scalar.copy(out=rows[:], in_=tiles["dx bank", g][:])
            b, n = divmod(g, GROUPS_PER_GRAPH)
            nc.sync.dma_start(out=out_0[b, 512 * n:512 * (n + 1), :].rearrange("(p t) w -> p t w", t=4), in_=rows[:])

        def w_transpose():
            bank = tpool.tile([P, 4, P], F32, name="ps")
            words = tiles["w"][:].bitcast(F32)
            for u in range(2):
                nc.tensor.transpose(bank[:, u, :], words[:, u:256:2], ident[:])
            tiles["w4"] = keep.tile([P, 4 * R], BF16, name="wi", align_bytes=64)
            nc.scalar.copy(out=tiles["w4"][:].bitcast(F32).rearrange("p (r u) -> p r u", u=2),
                           in_=bank[:, 0:2, :].rearrange("p u r -> p r u"))

        def w_quantize():
            nc.vector.quantize_mx(out=w_codes[:].bitcast(E4), scales=w_scales[:], in_=tiles["w4"][:])

        def dxw_interleave(g):
            tiles["dxw4", g] = work.tile([P, 4 * I], BF16, name="DI", bufs=2, align_bytes=64)
            nc.vector.tensor_copy(out=tiles["dxw4", g][:].rearrange("p (c i t) -> p c t i", i=4, t=4),
                                  in_=tiles["dxw", g][:].rearrange("p t (c i) -> p c t i", i=4))

        def dxw_interleave_half(g, half):
            if half == 0:
                tiles["dxw4", g] = work.tile([P, 4 * I], BF16, name="DI", bufs=2, align_bytes=64)
            out = tiles["dxw4", g][:, 1024 * half:1024 * (half + 1)]
            src = tiles["dxw", g][:, :, 256 * half:256 * (half + 1)]
            nc.vector.tensor_copy(out=out.rearrange("p (c i t) -> p c t i", i=4, t=4),
                                  in_=src.rearrange("p t (c i) -> p c t i", i=4))

        def dxw_quantize(g):
            codes = keep.tile([P, I], U32, name="tc%d" % g, align_bytes=64)
            scales = keep.tile([P, I], U8, name="ts%d" % g, align_bytes=64)
            nc.vector.quantize_mx(out=codes[:].bitcast(E5), scales=scales[:], in_=tiles["dxw4", g][:])
            tiles["dxw codes", g], tiles["dxw scales", g] = codes, scales

        def x_interleave(two):
            b, pair = divmod(two, 2)
            if pair == 0:
                tiles["x4", b] = work.tile([P, GROUPS_PER_GRAPH, R, 4], BF16, name="xi", tag="gi", bufs=2,
                                           align_bytes=64)
            for j in range(2):
                src = tiles["x"][:, 2 * two + j].rearrange("p t (c i) -> p c t i", i=4)
                out = tiles["x4", b][:, 2 * pair + j].rearrange("p (c i) t -> p c t i", i=4)
                nc.vector.tensor_copy(out=out, in_=src)

        def x_quantize(b):
            if b == 0:
                tiles["x codes"] = keep.tile([P, GROUPS * R], U32, name="xc", align_bytes=64)
                tiles["x scales"] = keep.tile([P, GROUPS * R], U8, name="xs", align_bytes=64)
            words = slice(GROUPS_PER_GRAPH * R * b, GROUPS_PER_GRAPH * R * (b + 1))
            nc.vector.quantize_mx(out=tiles["x codes"][:, words].bitcast(E4), scales=tiles["x scales"][:, words],
                                  in_=tiles["x4", b][:].rearrange("p g w t -> p (g w t)"))

        def dw_product(g):
            if g == 0:
                tiles["dw"] = apool.tile([P, I], F32, name="acc")
            cols = slice(R * g, R * (g + 1))
            nc.tensor.matmul_mx(out=tiles["dw"][:], lhsT=tiles["x codes"][:, cols].bitcast(E4),
                                lhsT_scale=tiles["x scales"][:, cols],
                                rhs=tiles["dxw codes", g][:].bitcast(E5), rhs_scale=tiles["dxw scales", g][:],
                                start=(g == 0), stop=(g == GROUPS - 1))

        def dw_store():
            rows = work.tile([P, I], F32, name="wo", bufs=1, align_bytes=64)
            nc.vector.tensor_copy(out=rows[:].rearrange("p (m u e) -> p m u e", u=2, e=2),
                                  in_=tiles["dw"][:].rearrange("p (u m e) -> p m u e", u=2, e=2))
            nc.sync.dma_start(out=out_1, in_=rows[:])

        load_dinv(0, 2, nc.scalar)
        load_grad(0, 0, parts=2)
        load_flows(0, (0, 1))
        load_grad(0, 1)
        load_dinv(2, 4, nc.sync)
        load_flows(0, (1, 2))
        load_grad(0, 2)
        load_flows(1, (0, 1))
        load_grad(0, 3)
        load_flows(1, (1, 2))
        load_dinv(4, 8, nc.sync)
        load_flows(2)
        load_w()

        gz_multiply(0, 0)
        gz_interleave_half(0, 0, 0, nc.vector.tensor_copy)
        gz_interleave_half(0, 0, 1, nc.scalar.copy)
        flows_transpose(0, 0)
        gz_multiply(0, 1)
        gz_quantize(0, 0)
        gz_interleave_half(0, 1, 0, nc.vector.tensor_copy)
        gz_interleave_half(0, 1, 1, nc.scalar.copy)
        flows_quantize(0, (0, 1))
        flows_transpose(0, 1)
        gz_multiply(0, 2)
        gz_quantize(0, 1)
        aggregate(0, 0, (0, 1))
        gz_interleave_half(0, 2, 0, nc.vector.tensor_copy)
        gz_interleave_half(0, 2, 1, nc.scalar.copy)
        flows_quantize(0, (1, 2))
        gz_multiply(0, 3)
        load_flows(3)
        load_grad(1, 0)
        load_flows(4)
        load_grad(1, 1)
        gz_quantize(0, 2)
        flows_transpose(1, 0)
        aggregate(0, 1, (0, 1))
        gz_interleave_half(0, 3, 0, nc.vector.tensor_copy)
        gz_interleave_half(0, 3, 1, nc.scalar.copy)
        flows_transpose(1, 1)
        aggregate(0, 0, (2,))
        aggregate(0, 1, (2,))
        flows_quantize(1, (0, 1))
        gz_quantize(0, 3)
        flows_sort(2)
        aggregate(0, 0, (3,))
        aggregate(0, 1, (3,))
        flows_quantize(1, (1, 2))
        aggregate(1, 0)
        flows_transpose(2, 0)
        dxw_rows(0, 0, on_vector=True)
        dxw_rows(0, 1, on_vector=True)
        flows_transpose(2, 1)
        dxw_rows(1, 0)
        flows_sort(3)
        gz_multiply(1, 0)
        aggregate(1, 1)
        w_transpose()
        flows_quantize(2)
        dxw_rows(1, 1)
        load_flows(5)

        vector_work = {
            3: [(flows_sort, 4), (gz_interleave, 1, 0), (flows_quantize, 3), (gz_multiply, 1, 1),
                (dxw_transpose_quantize, 0), (gz_quantize, 1, 0)],
            4: [(flows_sort, 5), (gz_interleave, 1, 1), (flows_quantize, 4), (dxw_interleave, 0)],
            5: [(flows_sort, 6), (gz_multiply, 1, 2), (gz_quantize, 1, 1), (flows_quantize, 5),
                (dxw_transpose_quantize, 1), (dxw_quantize, 0)],
            6: [(flows_sort, 7), (gz_interleave, 1, 2), (flows_quantize, 6), (gz_multiply, 1, 3), (gz_quantize, 1, 2)],
            7: [(flows_sort, 8), (gz_interleave, 1, 3), (flows_quantize, 7), (dxw_transpose_quantize, 2)],
            8: [(flows_sort, 9), (gz_quantize, 1, 3), (flows_quantize, 8), (dxw_interleave, 1)],
            9: [(flows_sort, 10), (dxw_quantize, 1), (flows_quantize, 9), (dxw_transpose_quantize, 3),
                (dxw_interleave, 2)],
            10: [(flows_sort, 11), (dxw_quantize, 2), (flows_quantize, 10), (dxw_interleave, 3)],
            11: [(flows_sort, 12), (dxw_quantize, 3), (flows_quantize, 11), (dxw_transpose_quantize, 4)],
            12: [(dxw_interleave, 4), (flows_sort, 13), (flows_quantize, 12), (dxw_quantize, 4)],
            13: [(flows_sort, 14), (x_interleave, 0), (flows_quantize, 13), (dxw_transpose_quantize, 5),
                 (x_interleave, 1)],
            14: [(dxw_interleave, 5), (flows_sort, 15), (x_quantize, 0), (flows_quantize, 14), (dxw_quantize, 5)],
            15: [(x_interleave, 2), (x_interleave, 3), (flows_quantize, 15), (x_quantize, 1),
                 (dxw_transpose_quantize, 6)],
        }
        for k in range(3, STEPS):
            if k + 3 < STEPS:
                load_flows(k + 3)
            elif k + 3 == STEPS:
                load_x()
            if k == 3:
                load_grad(1, 2)
                load_grad(1, 3)

            flows_transpose(k, 0)
            flows_transpose(k, 1)
            for j in (0, 1) if k == 3 else (k - 2,):
                dxw_transpose(j)
                dxw_transpose_copy(j)
            if k % 2 == 1 and k > 3:
                dx_transpose((k - 5) // 2)
                dx_store((k - 5) // 2)
            if k % 2 == 0:
                dx_product((k - 4) // 2)
                dx_copy((k - 4) // 2)
            for s in range(2):
                aggregate(k - 1, s)
                dxw_rows(k - 1, s)

            if k == 3:
                w_quantize()
            for call, *arguments in vector_work[k]:
                call(*arguments)

        last = GROUPS - 1
        for s in range(2):
            aggregate(STEPS - 1, s)
            dxw_rows(STEPS - 1, s)
        dxw_interleave(last - 1)
        dxw_quantize(last - 1)
        dxw_transpose(STEPS - 2)
        dxw_transpose_copy(STEPS - 2)
        dxw_transpose(STEPS - 1, (0,))
        dx_product(last - 1)
        dxw_transpose(STEPS - 1, (1,))
        dxw_transpose_copy(STEPS - 1)
        dx_copy(last - 1)
        dxw_interleave_half(last, 0)
        dxw_transpose_quantize(last)
        dxw_interleave_half(last, 1)
        for g in range(4):
            dw_product(g)
        dx_product(last)
        dx_copy(last)
        dx_transpose(last - 1)
        dx_store(last - 1)
        dw_product(4)
        dxw_quantize(last)
        dx_transpose(last)
        dx_store(last)
        for g in range(5, GROUPS):
            dw_product(g)
        dw_store()
